import numpy as np
import ml_dtypes


def mxq(x, axis, fmt="e4m3"):
    dtype, down = {"e4m3": (ml_dtypes.float8_e4m3fn, 7), "e5m2": (ml_dtypes.float8_e5m2, 14)}[fmt]
    v = np.moveaxis(np.asarray(x, np.float32).astype(ml_dtypes.bfloat16).astype(np.float64), axis, -1)
    blocks = v.reshape(v.shape[:-1] + (-1, 32))
    amax = np.abs(blocks).max(-1, keepdims=True)
    byte = np.maximum(np.where(amax > 0, np.frexp(amax)[1] - 1 + 127, 0) - down, 1)
    scale = np.exp2(byte - 127.0)
    codes = (blocks / scale).astype(np.float32).astype(dtype).astype(np.float64)
    return np.moveaxis((codes * scale).reshape(v.shape), -1, axis)


WIDE = False


def mx_kscale(k):
    if not WIDE:
        return np.ones(k)
    levels = np.array([10, -10, 5, -5, 0])
    a = np.random.permutation(np.resize(levels, k // 512 * 4)).reshape(k // 512, 4)
    idx = np.arange(k)
    return np.exp2(a[idx // 512, idx % 128 // 32])


BF16 = ml_dtypes.bfloat16


def bf(x):
    return np.asarray(x, np.float32).astype(BF16)


def f64(x):
    return np.asarray(x).astype(np.float64)


B, I, R, O = 16, 8, 64, 8
K = I * R
N = R * O


def setup_inputs():
    s = mx_kscale(K).reshape(I, R)
    v = mx_kscale(K)[:R]
    return {"t_first": bf(np.random.standard_normal((B, I, I, I, R, O)) * s[None, :, None, None, :, None]),
            "mid_core0": bf(np.random.standard_normal((I, R, R, O)) / np.sqrt(K) / s[:, :, None, None] * v[None, None, :, None]),
            "mid_core1": bf(np.random.standard_normal((I, R, R, O)) / np.sqrt(K) / v[None, :, None, None])}


def reference(t_first, mid_core0, mid_core1):
    a = f64(t_first).transpose(0, 2, 3, 5, 1, 4).reshape(B * I * I * O, K)
    t = mxq(a, 1, "e4m3") @ mxq(f64(mid_core0).reshape(K, N), 0, "e4m3")
    t = t.reshape(B, I, I, O, R, O)
    a = t.transpose(0, 2, 3, 5, 1, 4).reshape(B * I * O * O, K)
    t = mxq(a, 1, "e4m3") @ mxq(f64(mid_core1).reshape(K, N), 0, "e4m3")
    return t.reshape(B, I, O, O, R, O)

@@ -1,0 +1,200 @@
+from contextlib import ExitStack
+
+import concourse.mybir as mybir
+from concourse.masks import make_identity
+
+BF16 = mybir.dt.bfloat16
+F32 = mybir.dt.float32
+U32 = mybir.dt.uint32
+U8 = mybir.dt.uint8
+FP8X4 = mybir.dt.float8_e4m3fn_x4
+
+P = 128
+PACK = 4
+B = 16
+SITE = 8
+BOND = 64
+PHYS = 8
+COLS = BOND * PHYS
+Y_HALVES = SITE // PACK
+P_PAIRS = PHYS // 2
+O_WORDS = PHYS // 2
+B_PAIR = 2
+CHUNKS = B // B_PAIR
+BZ = B_PAIR * SITE
+
+FLOPS = 2 * 2 * (B * SITE * SITE * PHYS) * (SITE * BOND) * COLS
+
+
+def tile_mpolinear2_pa_kernel(tc, t_first, mid_core0, mid_core1, out):
+    nc = tc.nc
+    with ExitStack() as ctx:
+        keep = ctx.enter_context(tc.tile_pool(name="keep", bufs=1))
+        work = ctx.enter_context(tc.tile_pool(name="work", bufs=2))
+        results = ctx.enter_context(tc.tile_pool(name="results", bufs=3))
+        psum_t = ctx.enter_context(tc.psum_pool(name="psum_t", bufs=2))
+        psum_1 = ctx.enter_context(tc.psum_pool(name="psum_1", bufs=3))
+        psum_2 = ctx.enter_context(tc.psum_pool(name="psum_2", bufs=3))
+
+        def copy_out(on_vector, dst, src):
+            if on_vector:
+                nc.vector.tensor_copy(out=dst, in_=src)
+            else:
+                nc.scalar.copy(out=dst, in_=src)
+
+        def load_chunk(chunk):
+            x_tile = keep.tile([P, SITE, COLS], BF16, name="x_tile%d" % chunk)
+            for bl in range(B_PAIR):
+                nc.sync.dma_start(
+                    out=x_tile[bl:P:B_PAIR],
+                    in_=t_first[B_PAIR * chunk + bl].rearrange("x y z r o -> (y z) x (r o)"),
+                )
+            return x_tile
+
+        x_tiles = [load_chunk(0)]
+        w0_raw = keep.tile([P, PACK, COLS], BF16)
+        nc.sync.dma_start(
+            out=w0_raw[:],
+            in_=mid_core0.rearrange("(t xl) r s p -> (xl r) t (s p)", t=PACK),
+        )
+        w1_raw = keep.tile([P, SITE, COLS], BF16)
+        for ph in range(2):
+            nc.sync.dma_start(
+                out=w1_raw[ph * BOND : (ph + 1) * BOND],
+                in_=mid_core1.rearrange("y s u q -> s y (u q)"),
+            )
+        for chunk in range(1, CHUNKS):
+            x_tiles.append(load_chunk(chunk))
+
+        ident = keep.tile([P, P], F32)
+        make_identity(nc, ident[:])
+        reorder = keep.tile([P, P], F32)
+        nc.vector.tensor_copy(
+            out=reorder[:].rearrange("i (b z y) -> i b z y", b=B_PAIR, z=SITE),
+            in_=ident[:].rearrange("i (y z b) -> i b z y", b=B_PAIR, z=SITE),
+        )
+
+        w0_grouped = keep.tile([P, PHYS, BOND, PACK], BF16, align_bytes=64)
+        nc.vector.tensor_copy(
+            out=w0_grouped[:], in_=w0_raw[:].rearrange("c t (s p) -> c p s t", p=PHYS)
+        )
+        w0_codes = keep.tile([P, COLS], U32, align_bytes=64)
+        w0_scales = keep.tile([P, COLS], U8, align_bytes=64)
+        nc.vector.quantize_mx(
+            out=w0_codes[:].bitcast(FP8X4),
+            scales=w0_scales[:],
+            in_=w0_grouped[:].rearrange("c p s t -> c (p s t)"),
+        )
+
+        w1_codes = []
+        w1_scales = []
+        for ph in range(2):
+            live = slice(ph * BOND, (ph + 1) * BOND)
+            dead = slice((1 - ph) * BOND, (2 - ph) * BOND)
+            w1_grouped = keep.tile(
+                [P, Y_HALVES, COLS, PACK], BF16, align_bytes=64, name="w1_grouped%d" % ph
+            )
+            nc.gpsimd.memset(
+                w1_grouped[dead].rearrange("m h n l -> m (h n l)").bitcast(F32), 0.0
+            )
+            copy_out(
+                ph == 1,
+                w1_grouped[live],
+                w1_raw[live].rearrange("m (h l) n -> m h n l", l=PACK),
+            )
+            codes = keep.tile([P, Y_HALVES, COLS], U32, align_bytes=64, name="w1_codes%d" % ph)
+            scales = keep.tile([P, Y_HALVES, COLS], U8, align_bytes=64, name="w1_scales%d" % ph)
+            nc.vector.quantize_mx(
+                out=codes[:].rearrange("m h n -> m (h n)").bitcast(FP8X4),
+                scales=scales[:].rearrange("m h n -> m (h n)"),
+                in_=w1_grouped[:].rearrange("m h n l -> m (h n l)"),
+            )
+            w1_codes.append(codes)
+            w1_scales.append(scales)
+
+        def transpose_and_quantise(chunk):
+            words = x_tiles[chunk][:].bitcast(F32).rearrange("g x (r w) -> g w (x r)", w=O_WORDS)
+            a_grouped = work.tile(
+                [P, Y_HALVES, BZ, O_WORDS, PACK * 2, PACK], BF16, align_bytes=64
+            )
+            for ow in range(O_WORDS):
+                bank = psum_t.tile([P, PACK, P], F32)
+                for t in range(PACK):
+                    nc.tensor.transpose(bank[:, t, :], words[:, ow, t * P : (t + 1) * P], reorder[:])
+                halves = bank[:].bitcast(BF16).rearrange(
+                    "c t (b h m) -> c h b m t", b=BZ, h=Y_HALVES
+                )
+                for yh in range(Y_HALVES):
+                    copy_out(ow % 2 == 0, a_grouped[:, yh, :, ow, :, :], halves[:, yh])
+            a_codes = work.tile([P, Y_HALVES, COLS], U32, align_bytes=64)
+            a_scales = work.tile([P, Y_HALVES, COLS], U8, align_bytes=64)
+            for yh in range(Y_HALVES):
+                nc.vector.quantize_mx(
+                    out=a_codes[:, yh, :].bitcast(FP8X4),
+                    scales=a_scales[:, yh, :],
+                    in_=a_grouped[:, yh].rearrange("c b w m t -> c (b w m t)"),
+                )
+            return a_codes, a_scales
+
+        def stage_1(a_codes, a_scales):
+            t2_grouped = work.tile([P, Y_HALVES, P_PAIRS, COLS], BF16, align_bytes=64)
+            t2_codes = work.tile([P, Y_HALVES, P_PAIRS, P], U32, align_bytes=64)
+            t2_scales = work.tile([P, Y_HALVES, P_PAIRS, P], U8, align_bytes=64)
+            for yh in range(Y_HALVES):
+                for pp in range(P_PAIRS):
+                    bank = psum_1.tile([P, COLS], F32)
+                    nc.tensor.matmul_mx(
+                        out=bank[:],
+                        lhsT=w0_codes[:, pp * P : (pp + 1) * P].bitcast(FP8X4),
+                        lhsT_scale=w0_scales[:, pp * P : (pp + 1) * P],
+                        rhs=a_codes[:, yh, :].bitcast(FP8X4),
+                        rhs_scale=a_scales[:, yh, :],
+                        start=True,
+                        stop=True,
+                    )
+                    copy_out(
+                        (yh * P_PAIRS + pp) % 3 == 0,
+                        t2_grouped[:, yh, pp, :].rearrange("m (g e l) -> m g e l", e=2, l=PACK),
+                        bank[:].rearrange("m (g l e) -> m g e l", l=PACK, e=2),
+                    )
+                nc.vector.quantize_mx(
+                    out=t2_codes[:, yh].rearrange("m a n -> m (a n)").bitcast(FP8X4),
+                    scales=t2_scales[:, yh].rearrange("m a n -> m (a n)"),
+                    in_=t2_grouped[:, yh].rearrange("m a n -> m (a n)"),
+                )
+            return t2_codes, t2_scales
+
+        def stage_2(chunk, t2_codes, t2_scales):
+            result = results.tile([P, PHYS, COLS], F32)
+            for p in range(PHYS):
+                pp, ph = divmod(p, 2)
+                acc = psum_2.tile([P, COLS], F32)
+                for yh in range(Y_HALVES):
+                    nc.tensor.matmul_mx(
+                        out=acc[:],
+                        lhsT=t2_codes[:, yh, pp, :].bitcast(FP8X4),
+                        lhsT_scale=t2_scales[:, yh, pp, :],
+                        rhs=w1_codes[ph][:, yh, :].bitcast(FP8X4),
+                        rhs_scale=w1_scales[ph][:, yh, :],
+                        start=(yh == 0),
+                        stop=(yh == Y_HALVES - 1),
+                    )
+                copy_out(p % 3 == 0, result[:, p, :], acc[:])
+            half = PHYS // 2
+            for first in (0, half):
+                nc.sync.dma_start(
+                    out=out[
+                        B_PAIR * chunk : B_PAIR * (chunk + 1), :, :, first : first + half
+                    ].rearrange("b z o p u q -> (b z o) (p u q)"),
+                    in_=result[:, first : first + half, :].rearrange("m p n -> m (p n)"),
+                )
+
+        a_ready = {}
+        t2_ready = {}
+        for step in range(CHUNKS + 2):
+            if step < CHUNKS:
+                a_ready[step] = transpose_and_quantise(step)
+            if 1 <= step <= CHUNKS:
+                t2_ready[step - 1] = stage_1(a_ready[step - 1][0], a_ready[step - 1][1])
+            if step >= 2:
+                stage_2(step - 2, t2_ready[step - 2][0], t2_ready[step - 2][1])

@@ -5,6 +5,7 @@ from concourse.masks import make_identity
 
 BF16 = mybir.dt.bfloat16
 F32 = mybir.dt.float32
+I32 = mybir.dt.int32
 U32 = mybir.dt.uint32
 U8 = mybir.dt.uint8
 FP8X4 = mybir.dt.float8_e4m3fn_x4
@@ -16,12 +17,15 @@ SITE = 8
 BOND = 64
 PHYS = 8
 COLS = BOND * PHYS
+PSUM_BANKS = 8
 Y_HALVES = SITE // PACK
 P_PAIRS = PHYS // 2
 O_WORDS = PHYS // 2
 B_PAIR = 2
 CHUNKS = B // B_PAIR
 BZ = B_PAIR * SITE
+UNITS = CHUNKS * P_PAIRS
+STAGE_2_LAG = 3
 
 FLOPS = 2 * 2 * (B * SITE * SITE * PHYS) * (SITE * BOND) * COLS
 
@@ -29,12 +33,11 @@ FLOPS = 2 * 2 * (B * SITE * SITE * PHYS) * (SITE * BOND) * COLS
 def tile_mpolinear2_pa_kernel(tc, t_first, mid_core0, mid_core1, out):
     nc = tc.nc
     with ExitStack() as ctx:
+        ctx.enter_context(tc.manual_schedule())
         keep = ctx.enter_context(tc.tile_pool(name="keep", bufs=1))
-        work = ctx.enter_context(tc.tile_pool(name="work", bufs=2))
-        results = ctx.enter_context(tc.tile_pool(name="results", bufs=3))
-        psum_t = ctx.enter_context(tc.psum_pool(name="psum_t", bufs=2))
-        psum_1 = ctx.enter_context(tc.psum_pool(name="psum_1", bufs=3))
-        psum_2 = ctx.enter_context(tc.psum_pool(name="psum_2", bufs=3))
+        per_chunk = ctx.enter_context(tc.tile_pool(name="per_chunk", bufs=2))
+        per_unit = ctx.enter_context(tc.tile_pool(name="per_unit", bufs=STAGE_2_LAG + 3))
+        psum = ctx.enter_context(tc.psum_pool(name="psum", bufs=PSUM_BANKS))
 
         def copy_out(on_vector, dst, src):
             if on_vector:
@@ -51,12 +54,12 @@ def tile_mpolinear2_pa_kernel(tc, t_first, mid_core0, mid_core1, out):
                 )
             return x_tile
 
-        x_tiles = [load_chunk(0)]
         w0_raw = keep.tile([P, PACK, COLS], BF16)
         nc.sync.dma_start(
             out=w0_raw[:],
             in_=mid_core0.rearrange("(t xl) r s p -> (xl r) t (s p)", t=PACK),
         )
+        x_tiles = [load_chunk(0)]
         w1_raw = keep.tile([P, SITE, COLS], BF16)
         for ph in range(2):
             nc.sync.dma_start(
@@ -74,6 +77,12 @@ def tile_mpolinear2_pa_kernel(tc, t_first, mid_core0, mid_core1, out):
             in_=ident[:].rearrange("i (y z b) -> i b z y", b=B_PAIR, z=SITE),
         )
 
+        w1_codes = []
+        for ph in range(2):
+            codes = keep.tile([P, Y_HALVES, COLS], U32, align_bytes=64, name="w1_codes%d" % ph)
+            nc.vector.memset(codes[(1 - ph) * BOND : (2 - ph) * BOND].bitcast(I32), 0)
+            w1_codes.append(codes)
+
         w0_grouped = keep.tile([P, PHYS, BOND, PACK], BF16, align_bytes=64)
         nc.vector.tensor_copy(
             out=w0_grouped[:], in_=w0_raw[:].rearrange("c t (s p) -> c p s t", p=PHYS)
@@ -86,115 +95,131 @@ def tile_mpolinear2_pa_kernel(tc, t_first, mid_core0, mid_core1, out):
             in_=w0_grouped[:].rearrange("c p s t -> c (p s t)"),
         )
 
-        w1_codes = []
-        w1_scales = []
-        for ph in range(2):
-            live = slice(ph * BOND, (ph + 1) * BOND)
-            dead = slice((1 - ph) * BOND, (2 - ph) * BOND)
-            w1_grouped = keep.tile(
-                [P, Y_HALVES, COLS, PACK], BF16, align_bytes=64, name="w1_grouped%d" % ph
+        w1_scales = keep.tile([P, Y_HALVES, COLS], U8, align_bytes=64)
+
+        def prepare_core1():
+            w1_grouped = keep.tile([P, Y_HALVES, COLS, PACK], BF16, align_bytes=64)
+            nc.vector.tensor_copy(
+                out=w1_grouped[:], in_=w1_raw[:].rearrange("m (h l) n -> m h n l", l=PACK)
             )
-            nc.gpsimd.memset(
-                w1_grouped[dead].rearrange("m h n l -> m (h n l)").bitcast(F32), 0.0
-            )
-            copy_out(
-                ph == 1,
-                w1_grouped[live],
-                w1_raw[live].rearrange("m (h l) n -> m h n l", l=PACK),
-            )
-            codes = keep.tile([P, Y_HALVES, COLS], U32, align_bytes=64, name="w1_codes%d" % ph)
-            scales = keep.tile([P, Y_HALVES, COLS], U8, align_bytes=64, name="w1_scales%d" % ph)
+            w1_both = keep.tile([P, Y_HALVES, COLS], U32, align_bytes=64)
             nc.vector.quantize_mx(
-                out=codes[:].rearrange("m h n -> m (h n)").bitcast(FP8X4),
-                scales=scales[:].rearrange("m h n -> m (h n)"),
+                out=w1_both[:].rearrange("m h n -> m (h n)").bitcast(FP8X4),
+                scales=w1_scales[:].rearrange("m h n -> m (h n)"),
                 in_=w1_grouped[:].rearrange("m h n l -> m (h n l)"),
             )
-            w1_codes.append(codes)
-            w1_scales.append(scales)
+            for ph in range(2):
+                live = slice(ph * BOND, (ph + 1) * BOND)
+                nc.vector.tensor_copy(
+                    out=w1_codes[ph][live].bitcast(I32), in_=w1_both[live].bitcast(I32)
+                )
 
-        def transpose_and_quantise(chunk):
+        a_grouped = {}
+        a_codes = {}
+        a_scales = {}
+
+        def transpose_chunk(chunk):
             words = x_tiles[chunk][:].bitcast(F32).rearrange("g x (r w) -> g w (x r)", w=O_WORDS)
-            a_grouped = work.tile(
-                [P, Y_HALVES, BZ, O_WORDS, PACK * 2, PACK], BF16, align_bytes=64
+            grouped = per_chunk.tile(
+                [P, Y_HALVES, BZ, O_WORDS, PACK * 2, PACK], BF16, align_bytes=64, name="a_grouped"
             )
+            banks = []
             for ow in range(O_WORDS):
-                bank = psum_t.tile([P, PACK, P], F32)
+                bank = psum.tile([P, PACK, P], F32, tag="bank")
                 for t in range(PACK):
                     nc.tensor.transpose(bank[:, t, :], words[:, ow, t * P : (t + 1) * P], reorder[:])
-                halves = bank[:].bitcast(BF16).rearrange(
+                banks.append(bank)
+            for ow in range(O_WORDS):
+                halves = banks[ow][:].bitcast(BF16).rearrange(
                     "c t (b h m) -> c h b m t", b=BZ, h=Y_HALVES
                 )
                 for yh in range(Y_HALVES):
-                    copy_out(ow % 2 == 0, a_grouped[:, yh, :, ow, :, :], halves[:, yh])
-            a_codes = work.tile([P, Y_HALVES, COLS], U32, align_bytes=64)
-            a_scales = work.tile([P, Y_HALVES, COLS], U8, align_bytes=64)
+                    copy_out(ow % 2 == 0, grouped[:, yh, :, ow, :, :], halves[:, yh])
+            a_grouped[chunk] = grouped
+
+        def quantise_a(chunk):
+            codes = per_chunk.tile([P, Y_HALVES, COLS], U32, align_bytes=64, name="a_codes")
+            scales = per_chunk.tile([P, Y_HALVES, COLS], U8, align_bytes=64, name="a_scales")
             for yh in range(Y_HALVES):
                 nc.vector.quantize_mx(
-                    out=a_codes[:, yh, :].bitcast(FP8X4),
-                    scales=a_scales[:, yh, :],
-                    in_=a_grouped[:, yh].rearrange("c b w m t -> c (b w m t)"),
+                    out=codes[:, yh, :].bitcast(FP8X4),
+                    scales=scales[:, yh, :],
+                    in_=a_grouped[chunk][:, yh].rearrange("c b w m t -> c (b w m t)"),
                 )
-            return a_codes, a_scales
+            a_codes[chunk] = codes
+            a_scales[chunk] = scales
 
-        def stage_1(a_codes, a_scales):
-            t2_grouped = work.tile([P, Y_HALVES, P_PAIRS, COLS], BF16, align_bytes=64)
-            t2_codes = work.tile([P, Y_HALVES, P_PAIRS, P], U32, align_bytes=64)
-            t2_scales = work.tile([P, Y_HALVES, P_PAIRS, P], U8, align_bytes=64)
+        t2_grouped = {}
+        t2_codes = {}
+        t2_scales = {}
+
+        def stage_1(unit):
+            chunk, pp = divmod(unit, P_PAIRS)
+            grouped = per_unit.tile([P, Y_HALVES, COLS], BF16, align_bytes=64, name="t2_grouped")
             for yh in range(Y_HALVES):
-                for pp in range(P_PAIRS):
-                    bank = psum_1.tile([P, COLS], F32)
-                    nc.tensor.matmul_mx(
-                        out=bank[:],
-                        lhsT=w0_codes[:, pp * P : (pp + 1) * P].bitcast(FP8X4),
-                        lhsT_scale=w0_scales[:, pp * P : (pp + 1) * P],
-                        rhs=a_codes[:, yh, :].bitcast(FP8X4),
-                        rhs_scale=a_scales[:, yh, :],
-                        start=True,
-                        stop=True,
-                    )
-                    copy_out(
-                        (yh * P_PAIRS + pp) % 3 == 0,
-                        t2_grouped[:, yh, pp, :].rearrange("m (g e l) -> m g e l", e=2, l=PACK),
-                        bank[:].rearrange("m (g l e) -> m g e l", l=PACK, e=2),
-                    )
-                nc.vector.quantize_mx(
-                    out=t2_codes[:, yh].rearrange("m a n -> m (a n)").bitcast(FP8X4),
-                    scales=t2_scales[:, yh].rearrange("m a n -> m (a n)"),
-                    in_=t2_grouped[:, yh].rearrange("m a n -> m (a n)"),
+                bank = psum.tile([P, COLS], F32, tag="bank")
+                nc.tensor.matmul_mx(
+                    out=bank[:],
+                    lhsT=w0_codes[:, pp * P : (pp + 1) * P].bitcast(FP8X4),
+                    lhsT_scale=w0_scales[:, pp * P : (pp + 1) * P],
+                    rhs=a_codes[chunk][:, yh, :].bitcast(FP8X4),
+                    rhs_scale=a_scales[chunk][:, yh, :],
+                    start=True,
+                    stop=True,
                 )
-            return t2_codes, t2_scales
+                copy_out(
+                    (Y_HALVES * pp + yh) % 3 == 0,
+                    grouped[:, yh, :].rearrange("m (g e l) -> m g e l", e=2, l=PACK),
+                    bank[:].rearrange("m (g l e) -> m g e l", l=PACK, e=2),
+                )
+            t2_grouped[unit] = grouped
 
-        def stage_2(chunk, t2_codes, t2_scales):
-            result = results.tile([P, PHYS, COLS], F32)
-            for p in range(PHYS):
-                pp, ph = divmod(p, 2)
-                acc = psum_2.tile([P, COLS], F32)
+        def quantise_t2(unit):
+            codes = per_unit.tile([P, Y_HALVES, P], U32, align_bytes=64, name="t2_codes")
+            scales = per_unit.tile([P, Y_HALVES, P], U8, align_bytes=64, name="t2_scales")
+            nc.vector.quantize_mx(
+                out=codes[:].rearrange("m h n -> m (h n)").bitcast(FP8X4),
+                scales=scales[:].rearrange("m h n -> m (h n)"),
+                in_=t2_grouped[unit][:].rearrange("m h n -> m (h n)"),
+            )
+            t2_codes[unit] = codes
+            t2_scales[unit] = scales
+
+        def stage_2(unit):
+            chunk, pp = divmod(unit, P_PAIRS)
+            result = per_unit.tile([P, 2, COLS], F32, name="result")
+            for ph in range(2):
+                acc = psum.tile([P, COLS], F32, tag="bank")
                 for yh in range(Y_HALVES):
                     nc.tensor.matmul_mx(
                         out=acc[:],
-                        lhsT=t2_codes[:, yh, pp, :].bitcast(FP8X4),
-                        lhsT_scale=t2_scales[:, yh, pp, :],
+                        lhsT=t2_codes[unit][:, yh, :].bitcast(FP8X4),
+                        lhsT_scale=t2_scales[unit][:, yh, :],
                         rhs=w1_codes[ph][:, yh, :].bitcast(FP8X4),
-                        rhs_scale=w1_scales[ph][:, yh, :],
+                        rhs_scale=w1_scales[:, yh, :],
                         start=(yh == 0),
                         stop=(yh == Y_HALVES - 1),
                     )
-                copy_out(p % 3 == 0, result[:, p, :], acc[:])
-            half = PHYS // 2
-            for first in (0, half):
-                nc.sync.dma_start(
-                    out=out[
-                        B_PAIR * chunk : B_PAIR * (chunk + 1), :, :, first : first + half
-                    ].rearrange("b z o p u q -> (b z o) (p u q)"),
-                    in_=result[:, first : first + half, :].rearrange("m p n -> m (p n)"),
-                )
+                copy_out((2 * pp + ph) % 3 == 0, result[:, ph, :], acc[:])
+            nc.sync.dma_start(
+                out=out[
+                    B_PAIR * chunk : B_PAIR * (chunk + 1), :, :, 2 * pp : 2 * pp + 2
+                ].rearrange("b z o p u q -> (b z o) (p u q)"),
+                in_=result[:].rearrange("m p n -> m (p n)"),
+            )
 
-        a_ready = {}
-        t2_ready = {}
-        for step in range(CHUNKS + 2):
-            if step < CHUNKS:
-                a_ready[step] = transpose_and_quantise(step)
-            if 1 <= step <= CHUNKS:
-                t2_ready[step - 1] = stage_1(a_ready[step - 1][0], a_ready[step - 1][1])
-            if step >= 2:
-                stage_2(step - 2, t2_ready[step - 2][0], t2_ready[step - 2][1])
+        transpose_chunk(0)
+        quantise_a(0)
+        prepare_core1()
+        for unit in range(UNITS + STAGE_2_LAG):
+            chunk, pp = divmod(unit, P_PAIRS)
+            if pp == 0 and chunk + 1 < CHUNKS:
+                transpose_chunk(chunk + 1)
+            if pp == 1 and chunk + 1 < CHUNKS:
+                quantise_a(chunk + 1)
+            if unit < UNITS:
+                stage_1(unit)
+            if 1 <= unit <= UNITS:
+                quantise_t2(unit - 1)
+            if unit >= STAGE_2_LAG:
+                stage_2(unit - STAGE_2_LAG)

@@ -11,6 +11,7 @@ U8 = mybir.dt.uint8
 FP8X4 = mybir.dt.float8_e4m3fn_x4
 
 P = 128
+HALF = P // 2
 PACK = 4
 B = 16
 SITE = 8
@@ -24,8 +25,13 @@ O_WORDS = PHYS // 2
 B_PAIR = 2
 CHUNKS = B // B_PAIR
 BZ = B_PAIR * SITE
-UNITS = CHUNKS * P_PAIRS
+STEP_PAIRS = 2
+STEPS_PER_CHUNK = P_PAIRS // STEP_PAIRS
+STEPS = CHUNKS * STEPS_PER_CHUNK
+SLOTS = 2 * STEP_PAIRS
+SLOT_WORDS = P + P // 4
 STAGE_2_LAG = 3
+LOADS_AHEAD = 3
 
 FLOPS = 2 * 2 * (B * SITE * SITE * PHYS) * (SITE * BOND) * COLS
 
@@ -36,14 +42,19 @@ def tile_mpolinear2_pa_kernel(tc, t_first, mid_core0, mid_core1, out):
         ctx.enter_context(tc.manual_schedule())
         keep = ctx.enter_context(tc.tile_pool(name="keep", bufs=1))
         per_chunk = ctx.enter_context(tc.tile_pool(name="per_chunk", bufs=2))
-        per_unit = ctx.enter_context(tc.tile_pool(name="per_unit", bufs=STAGE_2_LAG + 3))
+        per_step = ctx.enter_context(tc.tile_pool(name="per_step", bufs=STAGE_2_LAG + 2))
+        results = ctx.enter_context(tc.tile_pool(name="results", bufs=6))
         psum = ctx.enter_context(tc.psum_pool(name="psum", bufs=PSUM_BANKS))
+        low = slice(0, HALF)
+        high = slice(HALF, P)
 
         def copy_out(on_vector, dst, src):
             if on_vector:
                 nc.vector.tensor_copy(out=dst, in_=src)
             else:
                 nc.scalar.copy(out=dst, in_=src)
+
+        x_tiles = []
 
         def load_chunk(chunk):
             x_tile = keep.tile([P, SITE, COLS], BF16, name="x_tile%d" % chunk)
@@ -52,22 +63,21 @@ def tile_mpolinear2_pa_kernel(tc, t_first, mid_core0, mid_core1, out):
                     out=x_tile[bl:P:B_PAIR],
                     in_=t_first[B_PAIR * chunk + bl].rearrange("x y z r o -> (y z) x (r o)"),
                 )
-            return x_tile
+            x_tiles.append(x_tile)
 
         w0_raw = keep.tile([P, PACK, COLS], BF16)
         nc.sync.dma_start(
             out=w0_raw[:],
             in_=mid_core0.rearrange("(t xl) r s p -> (xl r) t (s p)", t=PACK),
         )
-        x_tiles = [load_chunk(0)]
-        w1_raw = keep.tile([P, SITE, COLS], BF16)
-        for ph in range(2):
-            nc.sync.dma_start(
-                out=w1_raw[ph * BOND : (ph + 1) * BOND],
-                in_=mid_core1.rearrange("y s u q -> s y (u q)"),
-            )
-        for chunk in range(1, CHUNKS):
-            x_tiles.append(load_chunk(chunk))
+        load_chunk(0)
+        w1_raw = keep.tile([P, Y_HALVES, PACK, COLS], BF16)
+        core1_rows = mid_core1.rearrange("(yh yl) s u q -> s yh yl (u q)", yl=PACK)
+        nc.sync.dma_start(out=w1_raw[low], in_=core1_rows)
+        for j in range(Y_HALVES):
+            nc.sync.dma_start(out=w1_raw[high, j], in_=core1_rows[:, 1 - j])
+        for chunk in range(1, LOADS_AHEAD):
+            load_chunk(chunk)
 
         ident = keep.tile([P, P], F32)
         make_identity(nc, ident[:])
@@ -77,42 +87,33 @@ def tile_mpolinear2_pa_kernel(tc, t_first, mid_core0, mid_core1, out):
             in_=ident[:].rearrange("i (y z b) -> i b z y", b=B_PAIR, z=SITE),
         )
 
-        w1_codes = []
-        for ph in range(2):
-            codes = keep.tile([P, Y_HALVES, COLS], U32, align_bytes=64, name="w1_codes%d" % ph)
-            nc.vector.memset(codes[(1 - ph) * BOND : (2 - ph) * BOND].bitcast(I32), 0)
-            w1_codes.append(codes)
+        w0_blocks = 3
+        w0_cols = P_PAIRS * w0_blocks * BOND
+        w0_grouped = keep.tile([P, P_PAIRS, w0_blocks, BOND, PACK], BF16, align_bytes=64)
+        w0_by_p = w0_raw[:].rearrange("c t (s pp ph) -> c pp ph s t", pp=P_PAIRS, ph=2)
+        for block in range(w0_blocks):
+            nc.vector.tensor_copy(out=w0_grouped[:, :, block], in_=w0_by_p[:, :, block % 2])
+        w0_codes = keep.tile([P, w0_cols], U32, align_bytes=64)
+        w0_scales = keep.tile([P, w0_cols], U8, align_bytes=64)
+        w0_flat = w0_grouped[:].rearrange("c a k s t -> c (a k s t)")
+        for first, width in ((0, COLS), (COLS, w0_cols - COLS)):
+            nc.vector.quantize_mx(
+                out=w0_codes[:, first : first + width].bitcast(FP8X4),
+                scales=w0_scales[:, first : first + width],
+                in_=w0_flat[:, PACK * first : PACK * (first + width)],
+            )
 
-        w0_grouped = keep.tile([P, PHYS, BOND, PACK], BF16, align_bytes=64)
-        nc.vector.tensor_copy(
-            out=w0_grouped[:], in_=w0_raw[:].rearrange("c t (s p) -> c p s t", p=PHYS)
-        )
-        w0_codes = keep.tile([P, COLS], U32, align_bytes=64)
-        w0_scales = keep.tile([P, COLS], U8, align_bytes=64)
-        nc.vector.quantize_mx(
-            out=w0_codes[:].bitcast(FP8X4),
-            scales=w0_scales[:],
-            in_=w0_grouped[:].rearrange("c p s t -> c (p s t)"),
-        )
-
+        w1_codes = keep.tile([P, Y_HALVES, COLS], U32, align_bytes=64)
         w1_scales = keep.tile([P, Y_HALVES, COLS], U8, align_bytes=64)
 
         def prepare_core1():
             w1_grouped = keep.tile([P, Y_HALVES, COLS, PACK], BF16, align_bytes=64)
-            nc.vector.tensor_copy(
-                out=w1_grouped[:], in_=w1_raw[:].rearrange("m (h l) n -> m h n l", l=PACK)
-            )
-            w1_both = keep.tile([P, Y_HALVES, COLS], U32, align_bytes=64)
+            nc.vector.tensor_copy(out=w1_grouped[:], in_=w1_raw[:].rearrange("m j l n -> m j n l"))
             nc.vector.quantize_mx(
-                out=w1_both[:].rearrange("m h n -> m (h n)").bitcast(FP8X4),
-                scales=w1_scales[:].rearrange("m h n -> m (h n)"),
-                in_=w1_grouped[:].rearrange("m h n l -> m (h n l)"),
+                out=w1_codes[:].rearrange("m j n -> m (j n)").bitcast(FP8X4),
+                scales=w1_scales[:].rearrange("m j n -> m (j n)"),
+                in_=w1_grouped[:].rearrange("m j n l -> m (j n l)"),
             )
-            for ph in range(2):
-                live = slice(ph * BOND, (ph + 1) * BOND)
-                nc.vector.tensor_copy(
-                    out=w1_codes[ph][live].bitcast(I32), in_=w1_both[live].bitcast(I32)
-                )
 
         a_grouped = {}
         a_codes = {}
@@ -150,76 +151,87 @@ def tile_mpolinear2_pa_kernel(tc, t_first, mid_core0, mid_core1, out):
             a_scales[chunk] = scales
 
         t2_grouped = {}
-        t2_codes = {}
-        t2_scales = {}
+        t2_merged = {}
 
-        def stage_1(unit):
-            chunk, pp = divmod(unit, P_PAIRS)
-            grouped = per_unit.tile([P, Y_HALVES, COLS], BF16, align_bytes=64, name="t2_grouped")
-            for yh in range(Y_HALVES):
+        def stage_1(step):
+            chunk, part = divmod(step, STEPS_PER_CHUNK)
+            grouped = per_step.tile([P, SLOTS, COLS], BF16, align_bytes=64, name="t2_grouped")
+            for slot in range(SLOTS):
+                pair, yh = divmod(slot, Y_HALVES)
+                pp = STEP_PAIRS * part + pair
+                first = (w0_blocks * pp + yh) * BOND
                 bank = psum.tile([P, COLS], F32, tag="bank")
                 nc.tensor.matmul_mx(
                     out=bank[:],
-                    lhsT=w0_codes[:, pp * P : (pp + 1) * P].bitcast(FP8X4),
-                    lhsT_scale=w0_scales[:, pp * P : (pp + 1) * P],
+                    lhsT=w0_codes[:, first : first + P].bitcast(FP8X4),
+                    lhsT_scale=w0_scales[:, first : first + P],
                     rhs=a_codes[chunk][:, yh, :].bitcast(FP8X4),
                     rhs_scale=a_scales[chunk][:, yh, :],
                     start=True,
                     stop=True,
                 )
                 copy_out(
-                    (Y_HALVES * pp + yh) % 3 == 0,
-                    grouped[:, yh, :].rearrange("m (g e l) -> m g e l", e=2, l=PACK),
+                    (SLOTS * part + slot) % 3 == 0,
+                    grouped[:, slot, :].rearrange("m (g e l) -> m g e l", e=2, l=PACK),
                     bank[:].rearrange("m (g l e) -> m g e l", l=PACK, e=2),
                 )
-            t2_grouped[unit] = grouped
+            t2_grouped[step] = grouped
 
-        def quantise_t2(unit):
-            codes = per_unit.tile([P, Y_HALVES, P], U32, align_bytes=64, name="t2_codes")
-            scales = per_unit.tile([P, Y_HALVES, P], U8, align_bytes=64, name="t2_scales")
-            nc.vector.quantize_mx(
-                out=codes[:].rearrange("m h n -> m (h n)").bitcast(FP8X4),
-                scales=scales[:].rearrange("m h n -> m (h n)"),
-                in_=t2_grouped[unit][:].rearrange("m h n -> m (h n)"),
-            )
-            t2_codes[unit] = codes
-            t2_scales[unit] = scales
+        def quantise_and_merge_t2(step):
+            split = per_step.tile([P, SLOTS, SLOT_WORDS], U32, align_bytes=64, name="t2_split")
+            for slot in range(SLOTS):
+                nc.vector.quantize_mx(
+                    out=split[:, slot, 0:P].bitcast(FP8X4),
+                    scales=split[:, slot, P:SLOT_WORDS].bitcast(U8),
+                    in_=t2_grouped[step][:, slot, :],
+                )
+            merged = per_step.tile([P, SLOTS, SLOT_WORDS], U32, align_bytes=64, name="t2_merged")
+            nc.sync.dma_start(out=merged[low].bitcast(I32), in_=split[low].bitcast(I32))
+            merged_pairs = merged[:].bitcast(I32).rearrange("m (a j) w -> m a j w", j=2)
+            split_pairs = split[:].bitcast(I32).rearrange("m (a j) w -> m a j w", j=2)
+            for j in range(2):
+                nc.sync.dma_start(out=merged_pairs[high, :, j], in_=split_pairs[high, :, 1 - j])
+            t2_merged[step] = merged
 
-        def stage_2(unit):
-            chunk, pp = divmod(unit, P_PAIRS)
-            result = per_unit.tile([P, 2, COLS], F32, name="result")
-            for ph in range(2):
-                acc = psum.tile([P, COLS], F32, tag="bank")
-                for yh in range(Y_HALVES):
+        def stage_2(step):
+            chunk, part = divmod(step, STEPS_PER_CHUNK)
+            for pair in range(STEP_PAIRS):
+                pp = STEP_PAIRS * part + pair
+                result = results.tile([P, 2, COLS], F32)
+                for j in range(2):
+                    slot = 2 * pair + j
+                    acc = psum.tile([P, COLS], F32, tag="bank")
                     nc.tensor.matmul_mx(
                         out=acc[:],
-                        lhsT=t2_codes[unit][:, yh, :].bitcast(FP8X4),
-                        lhsT_scale=t2_scales[unit][:, yh, :],
-                        rhs=w1_codes[ph][:, yh, :].bitcast(FP8X4),
-                        rhs_scale=w1_scales[:, yh, :],
-                        start=(yh == 0),
-                        stop=(yh == Y_HALVES - 1),
+                        lhsT=t2_merged[step][:, slot, 0:P].bitcast(FP8X4),
+                        lhsT_scale=t2_merged[step][:, slot, P:SLOT_WORDS].bitcast(U8),
+                        rhs=w1_codes[:, j, :].bitcast(FP8X4),
+                        rhs_scale=w1_scales[:, j, :],
+                        start=True,
+                        stop=True,
                     )
-                copy_out((2 * pp + ph) % 3 == 0, result[:, ph, :], acc[:])
-            nc.sync.dma_start(
-                out=out[
-                    B_PAIR * chunk : B_PAIR * (chunk + 1), :, :, 2 * pp : 2 * pp + 2
-                ].rearrange("b z o p u q -> (b z o) (p u q)"),
-                in_=result[:].rearrange("m p n -> m (p n)"),
-            )
+                    copy_out((2 * pp + j) % 3 == 0, result[:, j, :], acc[:])
+                nc.sync.dma_start(
+                    out=out[
+                        B_PAIR * chunk : B_PAIR * (chunk + 1), :, :, 2 * pp : 2 * pp + 2
+                    ].rearrange("b z o p u q -> (b z o) (p u q)"),
+                    in_=result[:].rearrange("m p n -> m (p n)"),
+                )
 
         transpose_chunk(0)
         quantise_a(0)
         prepare_core1()
-        for unit in range(UNITS + STAGE_2_LAG):
-            chunk, pp = divmod(unit, P_PAIRS)
-            if pp == 0 and chunk + 1 < CHUNKS:
+        for step in range(STEPS + STAGE_2_LAG):
+            chunk, part = divmod(step, STEPS_PER_CHUNK)
+            if part == 0 and chunk + LOADS_AHEAD < CHUNKS:
+                load_chunk(chunk + LOADS_AHEAD)
+            if part == 0 and chunk + 1 < CHUNKS:
                 transpose_chunk(chunk + 1)
-            if pp == 1 and chunk + 1 < CHUNKS:
+            if step < STEPS:
+                stage_1(step)
+            if part == 1 and chunk + 1 < CHUNKS:
                 quantise_a(chunk + 1)
-            if unit < UNITS:
-                stage_1(unit)
-            if 1 <= unit <= UNITS:
-                quantise_t2(unit - 1)
-            if unit >= STAGE_2_LAG:
-                stage_2(unit - STAGE_2_LAG)
+            if step >= STAGE_2_LAG:
+                stage_2(step - STAGE_2_LAG)
+            if step < STEPS:
+                quantise_and_merge_t2(step)

@@ -5,7 +5,6 @@ from concourse.masks import make_identity
 
 BF16 = mybir.dt.bfloat16
 F32 = mybir.dt.float32
-I32 = mybir.dt.int32
 U32 = mybir.dt.uint32
 U8 = mybir.dt.uint8
 FP8X4 = mybir.dt.float8_e4m3fn_x4
@@ -20,18 +19,15 @@ PHYS = 8
 COLS = BOND * PHYS
 PSUM_BANKS = 8
 Y_HALVES = SITE // PACK
-P_PAIRS = PHYS // 2
 O_WORDS = PHYS // 2
 B_PAIR = 2
 CHUNKS = B // B_PAIR
 BZ = B_PAIR * SITE
-STEP_PAIRS = 2
-STEPS_PER_CHUNK = P_PAIRS // STEP_PAIRS
-STEPS = CHUNKS * STEPS_PER_CHUNK
-SLOTS = 2 * STEP_PAIRS
-SLOT_WORDS = P + P // 4
-STAGE_2_LAG = 3
+UNITS = CHUNKS * PHYS
+STAGE_2_LAG = 2
 LOADS_AHEAD = 3
+RUN_BANKS = 2
+UNITS_PER_RUN = PHYS * RUN_BANKS // O_WORDS
 
 FLOPS = 2 * 2 * (B * SITE * SITE * PHYS) * (SITE * BOND) * COLS
 
@@ -42,11 +38,9 @@ def tile_mpolinear2_pa_kernel(tc, t_first, mid_core0, mid_core1, out):
         ctx.enter_context(tc.manual_schedule())
         keep = ctx.enter_context(tc.tile_pool(name="keep", bufs=1))
         per_chunk = ctx.enter_context(tc.tile_pool(name="per_chunk", bufs=2))
-        per_step = ctx.enter_context(tc.tile_pool(name="per_step", bufs=STAGE_2_LAG + 2))
+        per_unit = ctx.enter_context(tc.tile_pool(name="per_unit", bufs=STAGE_2_LAG + 2))
         results = ctx.enter_context(tc.tile_pool(name="results", bufs=6))
         psum = ctx.enter_context(tc.psum_pool(name="psum", bufs=PSUM_BANKS))
-        low = slice(0, HALF)
-        high = slice(HALF, P)
 
         def copy_out(on_vector, dst, src):
             if on_vector:
@@ -56,13 +50,17 @@ def tile_mpolinear2_pa_kernel(tc, t_first, mid_core0, mid_core1, out):
 
         x_tiles = []
 
-        def load_chunk(chunk):
+        def load_chunk(chunk, x_parts):
             x_tile = keep.tile([P, SITE, COLS], BF16, name="x_tile%d" % chunk)
-            for bl in range(B_PAIR):
-                nc.sync.dma_start(
-                    out=x_tile[bl:P:B_PAIR],
-                    in_=t_first[B_PAIR * chunk + bl].rearrange("x y z r o -> (y z) x (r o)"),
-                )
+            width = SITE // x_parts
+            for first in range(0, SITE, width):
+                for bl in range(B_PAIR):
+                    nc.sync.dma_start(
+                        out=x_tile[bl:P:B_PAIR, first : first + width],
+                        in_=t_first[B_PAIR * chunk + bl, first : first + width].rearrange(
+                            "x y z r o -> (y z) x (r o)"
+                        ),
+                    )
             x_tiles.append(x_tile)
 
         w0_raw = keep.tile([P, PACK, COLS], BF16)
@@ -70,168 +68,179 @@ def tile_mpolinear2_pa_kernel(tc, t_first, mid_core0, mid_core1, out):
             out=w0_raw[:],
             in_=mid_core0.rearrange("(t xl) r s p -> (xl r) t (s p)", t=PACK),
         )
-        load_chunk(0)
-        w1_raw = keep.tile([P, Y_HALVES, PACK, COLS], BF16)
-        core1_rows = mid_core1.rearrange("(yh yl) s u q -> s yh yl (u q)", yl=PACK)
-        nc.sync.dma_start(out=w1_raw[low], in_=core1_rows)
-        for j in range(Y_HALVES):
-            nc.sync.dma_start(out=w1_raw[high, j], in_=core1_rows[:, 1 - j])
+        load_chunk(0, 2)
+        w1_raw = keep.tile([P, PACK, COLS], BF16)
+        core1_rows = mid_core1.rearrange("(yh yl) s u q -> yh s yl (u q)", yl=PACK)
+        for yh in range(Y_HALVES):
+            nc.sync.dma_start(out=w1_raw[yh * HALF : (yh + 1) * HALF], in_=core1_rows[yh])
         for chunk in range(1, LOADS_AHEAD):
-            load_chunk(chunk)
+            load_chunk(chunk, 1)
+
+        w0_blocks = 2 * PHYS + 1
+        w0_codes = keep.tile([P, w0_blocks * BOND], U32, align_bytes=64)
+        w0_scales = keep.tile([P, w0_blocks * BOND], U8, align_bytes=64)
+        nc.vector.memset(w0_codes[:], 0)
+        nc.vector.memset(w0_scales[:].bitcast(U32), 0)
 
         ident = keep.tile([P, P], F32)
         make_identity(nc, ident[:])
         reorder = keep.tile([P, P], F32)
-        nc.vector.tensor_copy(
-            out=reorder[:].rearrange("i (b z y) -> i b z y", b=B_PAIR, z=SITE),
-            in_=ident[:].rearrange("i (y z b) -> i b z y", b=B_PAIR, z=SITE),
-        )
-
-        w0_blocks = 3
-        w0_cols = P_PAIRS * w0_blocks * BOND
-        w0_grouped = keep.tile([P, P_PAIRS, w0_blocks, BOND, PACK], BF16, align_bytes=64)
-        w0_by_p = w0_raw[:].rearrange("c t (s pp ph) -> c pp ph s t", pp=P_PAIRS, ph=2)
-        for block in range(w0_blocks):
-            nc.vector.tensor_copy(out=w0_grouped[:, :, block], in_=w0_by_p[:, :, block % 2])
-        w0_codes = keep.tile([P, w0_cols], U32, align_bytes=64)
-        w0_scales = keep.tile([P, w0_cols], U8, align_bytes=64)
-        w0_flat = w0_grouped[:].rearrange("c a k s t -> c (a k s t)")
-        for first, width in ((0, COLS), (COLS, w0_cols - COLS)):
-            nc.vector.quantize_mx(
-                out=w0_codes[:, first : first + width].bitcast(FP8X4),
-                scales=w0_scales[:, first : first + width],
-                in_=w0_flat[:, PACK * first : PACK * (first + width)],
+        for yh in range(Y_HALVES):
+            half = slice(yh * HALF, (yh + 1) * HALF)
+            nc.vector.tensor_copy(
+                out=reorder[:, half].rearrange("i (b z y) -> i b z y", b=B_PAIR, z=SITE),
+                in_=ident[:, half].rearrange("i (y z b) -> i b z y", b=B_PAIR, z=SITE),
             )
 
-        w1_codes = keep.tile([P, Y_HALVES, COLS], U32, align_bytes=64)
-        w1_scales = keep.tile([P, Y_HALVES, COLS], U8, align_bytes=64)
+        w0_grouped = keep.tile([P, PHYS, BOND, PACK], BF16, align_bytes=64)
+        nc.vector.tensor_copy(
+            out=w0_grouped[:], in_=w0_raw[:].rearrange("c t (s p) -> c p s t", p=PHYS)
+        )
+        for p in range(PHYS):
+            cols = slice((2 * p + 1) * BOND, (2 * p + 2) * BOND)
+            nc.vector.quantize_mx(
+                out=w0_codes[:, cols].bitcast(FP8X4),
+                scales=w0_scales[:, cols],
+                in_=w0_grouped[:, p].rearrange("c s t -> c (s t)"),
+            )
+
+        w1_codes = keep.tile([P, COLS], U32, align_bytes=64)
+        w1_scales = keep.tile([P, COLS], U8, align_bytes=64)
+        w1_grouped = keep.tile([P, COLS, PACK], BF16, align_bytes=64)
 
         def prepare_core1():
-            w1_grouped = keep.tile([P, Y_HALVES, COLS, PACK], BF16, align_bytes=64)
-            nc.vector.tensor_copy(out=w1_grouped[:], in_=w1_raw[:].rearrange("m j l n -> m j n l"))
+            nc.vector.tensor_copy(out=w1_grouped[:], in_=w1_raw[:].rearrange("m l n -> m n l"))
+
+        def quantise_core1():
             nc.vector.quantize_mx(
-                out=w1_codes[:].rearrange("m j n -> m (j n)").bitcast(FP8X4),
-                scales=w1_scales[:].rearrange("m j n -> m (j n)"),
-                in_=w1_grouped[:].rearrange("m j n l -> m (j n l)"),
+                out=w1_codes[:].bitcast(FP8X4),
+                scales=w1_scales[:],
+                in_=w1_grouped[:].rearrange("m n l -> m (n l)"),
             )
 
         a_grouped = {}
         a_codes = {}
         a_scales = {}
 
-        def transpose_chunk(chunk):
+        def transpose_run(chunk, run):
             words = x_tiles[chunk][:].bitcast(F32).rearrange("g x (r w) -> g w (x r)", w=O_WORDS)
-            grouped = per_chunk.tile(
-                [P, Y_HALVES, BZ, O_WORDS, PACK * 2, PACK], BF16, align_bytes=64, name="a_grouped"
-            )
             banks = []
-            for ow in range(O_WORDS):
-                bank = psum.tile([P, PACK, P], F32, tag="bank")
-                for t in range(PACK):
-                    nc.tensor.transpose(bank[:, t, :], words[:, ow, t * P : (t + 1) * P], reorder[:])
+            for i in range(RUN_BANKS):
+                bank = psum.tile([P, PACK, P], F32, tag="bank", name="bank")
                 banks.append(bank)
-            for ow in range(O_WORDS):
-                halves = banks[ow][:].bitcast(BF16).rearrange(
-                    "c t (b h m) -> c h b m t", b=BZ, h=Y_HALVES
-                )
-                for yh in range(Y_HALVES):
-                    copy_out(ow % 2 == 0, grouped[:, yh, :, ow, :, :], halves[:, yh])
-            a_grouped[chunk] = grouped
+            for t in range(PACK):
+                for i in range(RUN_BANKS):
+                    nc.tensor.transpose(
+                        banks[i][:, t, :], words[:, RUN_BANKS * run + i, t * P : (t + 1) * P], reorder[:]
+                    )
+            return banks
 
-        def quantise_a(chunk):
-            codes = per_chunk.tile([P, Y_HALVES, COLS], U32, align_bytes=64, name="a_codes")
-            scales = per_chunk.tile([P, Y_HALVES, COLS], U8, align_bytes=64, name="a_scales")
-            for yh in range(Y_HALVES):
-                nc.vector.quantize_mx(
-                    out=codes[:, yh, :].bitcast(FP8X4),
-                    scales=scales[:, yh, :],
-                    in_=a_grouped[chunk][:, yh].rearrange("c b w m t -> c (b w m t)"),
+        def regroup_run(chunk, run, banks):
+            if run == 0:
+                grouped = per_chunk.tile(
+                    [P, Y_HALVES * BZ, O_WORDS, PACK * 2, PACK], BF16, align_bytes=64, name="a_grouped"
                 )
-            a_codes[chunk] = codes
-            a_scales[chunk] = scales
+                a_grouped[chunk] = grouped
+            for i in range(RUN_BANKS):
+                copy_out(
+                    i % 2 == 1,
+                    a_grouped[chunk][:, :, RUN_BANKS * run + i],
+                    banks[i][:].bitcast(BF16).rearrange("c t (h m) -> c h m t", m=PACK * 2),
+                )
+
+        def quantise_a(chunk, yh):
+            if yh == 0:
+                codes = per_chunk.tile([P, Y_HALVES, COLS], U32, align_bytes=64, name="a_codes")
+                scales = per_chunk.tile([P, Y_HALVES, COLS], U8, align_bytes=64, name="a_scales")
+                a_codes[chunk] = codes
+                a_scales[chunk] = scales
+            nc.vector.quantize_mx(
+                out=a_codes[chunk][:, yh, :].bitcast(FP8X4),
+                scales=a_scales[chunk][:, yh, :],
+                in_=a_grouped[chunk][:, yh * BZ : (yh + 1) * BZ].rearrange("c b w m t -> c (b w m t)"),
+            )
 
         t2_grouped = {}
-        t2_merged = {}
+        t2_codes = {}
+        t2_scales = {}
+        result_tiles = {}
 
-        def stage_1(step):
-            chunk, part = divmod(step, STEPS_PER_CHUNK)
-            grouped = per_step.tile([P, SLOTS, COLS], BF16, align_bytes=64, name="t2_grouped")
-            for slot in range(SLOTS):
-                pair, yh = divmod(slot, Y_HALVES)
-                pp = STEP_PAIRS * part + pair
-                first = (w0_blocks * pp + yh) * BOND
-                bank = psum.tile([P, COLS], F32, tag="bank")
+        def stage_1(unit):
+            chunk, p = divmod(unit, PHYS)
+            bank = psum.tile([P, COLS], F32, tag="bank", name="bank")
+            for yh in range(Y_HALVES):
+                first = (2 * p + 1 - yh) * BOND
                 nc.tensor.matmul_mx(
                     out=bank[:],
                     lhsT=w0_codes[:, first : first + P].bitcast(FP8X4),
                     lhsT_scale=w0_scales[:, first : first + P],
                     rhs=a_codes[chunk][:, yh, :].bitcast(FP8X4),
                     rhs_scale=a_scales[chunk][:, yh, :],
-                    start=True,
-                    stop=True,
+                    start=yh == 0,
+                    stop=yh == Y_HALVES - 1,
                 )
-                copy_out(
-                    (SLOTS * part + slot) % 3 == 0,
-                    grouped[:, slot, :].rearrange("m (g e l) -> m g e l", e=2, l=PACK),
-                    bank[:].rearrange("m (g l e) -> m g e l", l=PACK, e=2),
-                )
-            t2_grouped[step] = grouped
+            grouped = per_unit.tile([P, COLS], BF16, align_bytes=64, name="t2_grouped")
+            nc.scalar.copy(
+                out=grouped[:].rearrange("m (g e l) -> m g e l", e=2, l=PACK),
+                in_=bank[:].rearrange("m (g l e) -> m g e l", l=PACK, e=2),
+            )
+            t2_grouped[unit] = grouped
 
-        def quantise_and_merge_t2(step):
-            split = per_step.tile([P, SLOTS, SLOT_WORDS], U32, align_bytes=64, name="t2_split")
-            for slot in range(SLOTS):
-                nc.vector.quantize_mx(
-                    out=split[:, slot, 0:P].bitcast(FP8X4),
-                    scales=split[:, slot, P:SLOT_WORDS].bitcast(U8),
-                    in_=t2_grouped[step][:, slot, :],
-                )
-            merged = per_step.tile([P, SLOTS, SLOT_WORDS], U32, align_bytes=64, name="t2_merged")
-            nc.sync.dma_start(out=merged[low].bitcast(I32), in_=split[low].bitcast(I32))
-            merged_pairs = merged[:].bitcast(I32).rearrange("m (a j) w -> m a j w", j=2)
-            split_pairs = split[:].bitcast(I32).rearrange("m (a j) w -> m a j w", j=2)
-            for j in range(2):
-                nc.sync.dma_start(out=merged_pairs[high, :, j], in_=split_pairs[high, :, 1 - j])
-            t2_merged[step] = merged
+        def quantise_t2(unit):
+            codes = per_unit.tile([P, P], U32, align_bytes=64, name="t2_codes")
+            scales = per_unit.tile([P, P], U8, align_bytes=64, name="t2_scales")
+            nc.vector.quantize_mx(out=codes[:].bitcast(FP8X4), scales=scales[:], in_=t2_grouped[unit][:])
+            t2_codes[unit] = codes
+            t2_scales[unit] = scales
 
-        def stage_2(step):
-            chunk, part = divmod(step, STEPS_PER_CHUNK)
-            for pair in range(STEP_PAIRS):
-                pp = STEP_PAIRS * part + pair
-                result = results.tile([P, 2, COLS], F32)
-                for j in range(2):
-                    slot = 2 * pair + j
-                    acc = psum.tile([P, COLS], F32, tag="bank")
-                    nc.tensor.matmul_mx(
-                        out=acc[:],
-                        lhsT=t2_merged[step][:, slot, 0:P].bitcast(FP8X4),
-                        lhsT_scale=t2_merged[step][:, slot, P:SLOT_WORDS].bitcast(U8),
-                        rhs=w1_codes[:, j, :].bitcast(FP8X4),
-                        rhs_scale=w1_scales[:, j, :],
-                        start=True,
-                        stop=True,
-                    )
-                    copy_out((2 * pp + j) % 3 == 0, result[:, j, :], acc[:])
+        def stage_2(unit):
+            chunk, p = divmod(unit, PHYS)
+            if p % 2 == 0:
+                result = results.tile([P, 2, COLS], F32, name="result")
+                result_tiles[unit // 2] = result
+            acc = psum.tile([P, COLS], F32, tag="bank", name="bank")
+            nc.tensor.matmul_mx(
+                out=acc[:],
+                lhsT=t2_codes[unit][:].bitcast(FP8X4),
+                lhsT_scale=t2_scales[unit][:],
+                rhs=w1_codes[:].bitcast(FP8X4),
+                rhs_scale=w1_scales[:],
+                start=True,
+                stop=True,
+            )
+            copy_out(p % 4 != 3, result_tiles[unit // 2][:, p % 2, :], acc[:])
+            if p % 2 == 1:
                 nc.sync.dma_start(
-                    out=out[
-                        B_PAIR * chunk : B_PAIR * (chunk + 1), :, :, 2 * pp : 2 * pp + 2
-                    ].rearrange("b z o p u q -> (b z o) (p u q)"),
-                    in_=result[:].rearrange("m p n -> m (p n)"),
+                    out=out[B_PAIR * chunk : B_PAIR * (chunk + 1), :, :, p - 1 : p + 1].rearrange(
+                        "b z o p u q -> (b z o) (p u q)"
+                    ),
+                    in_=result_tiles[unit // 2][:].rearrange("m p n -> m (p n)"),
                 )
 
-        transpose_chunk(0)
-        quantise_a(0)
+        runs = O_WORDS // RUN_BANKS
+        first_banks = [transpose_run(0, run) for run in range(runs)]
+        for run in range(runs):
+            regroup_run(0, run, first_banks[run])
+        quantise_a(0, 0)
+        quantise_a(0, 1)
         prepare_core1()
-        for step in range(STEPS + STAGE_2_LAG):
-            chunk, part = divmod(step, STEPS_PER_CHUNK)
-            if part == 0 and chunk + LOADS_AHEAD < CHUNKS:
-                load_chunk(chunk + LOADS_AHEAD)
-            if part == 0 and chunk + 1 < CHUNKS:
-                transpose_chunk(chunk + 1)
-            if step < STEPS:
-                stage_1(step)
-            if part == 1 and chunk + 1 < CHUNKS:
-                quantise_a(chunk + 1)
-            if step >= STAGE_2_LAG:
-                stage_2(step - STAGE_2_LAG)
-            if step < STEPS:
-                quantise_and_merge_t2(step)
+        for unit in range(UNITS + STAGE_2_LAG):
+            chunk, p = divmod(unit, PHYS)
+            has_next = chunk + 1 < CHUNKS
+            if p == 0 and chunk + LOADS_AHEAD < CHUNKS:
+                load_chunk(chunk + LOADS_AHEAD, 1)
+            run, at = divmod(p, UNITS_PER_RUN)
+            if at == 0 and has_next:
+                banks = transpose_run(chunk + 1, run)
+            if 1 <= unit <= UNITS:
+                quantise_t2(unit - 1)
+            if unit == 1:
+                quantise_core1()
+            if at == 0 and has_next:
+                regroup_run(chunk + 1, run, banks)
+            if unit < UNITS:
+                stage_1(unit)
+            if unit >= STAGE_2_LAG:
+                stage_2(unit - STAGE_2_LAG)
+            if UNITS_PER_RUN < p <= UNITS_PER_RUN + Y_HALVES and has_next:
+                quantise_a(chunk + 1, p - UNITS_PER_RUN - 1)

@@ -12,6 +12,7 @@ FP8X4 = mybir.dt.float8_e4m3fn_x4
 P = 128
 HALF = P // 2
 PACK = 4
+PAIR = 2
 B = 16
 SITE = 8
 BOND = 64
@@ -19,15 +20,18 @@ PHYS = 8
 COLS = BOND * PHYS
 PSUM_BANKS = 8
 Y_HALVES = SITE // PACK
-O_WORDS = PHYS // 2
+O_HALVES = 2
+O_RUN = PHYS // O_HALVES
+O_PAIRS = PHYS // PAIR
+BANKS_PER_RUN = O_PAIRS // O_HALVES
 B_PAIR = 2
 CHUNKS = B // B_PAIR
 BZ = B_PAIR * SITE
-UNITS = CHUNKS * PHYS
-STAGE_2_LAG = 2
+P_PAIR = 2
+STEPS_PER_CHUNK = PHYS // P_PAIR
+STEPS = CHUNKS * STEPS_PER_CHUNK
+STAGE_2_LAG = 1
 LOADS_AHEAD = 3
-RUN_BANKS = 2
-UNITS_PER_RUN = PHYS * RUN_BANKS // O_WORDS
 
 FLOPS = 2 * 2 * (B * SITE * SITE * PHYS) * (SITE * BOND) * COLS
 
@@ -38,11 +42,11 @@ def tile_mpolinear2_pa_kernel(tc, t_first, mid_core0, mid_core1, out):
         ctx.enter_context(tc.manual_schedule())
         keep = ctx.enter_context(tc.tile_pool(name="keep", bufs=1))
         per_chunk = ctx.enter_context(tc.tile_pool(name="per_chunk", bufs=2))
-        per_unit = ctx.enter_context(tc.tile_pool(name="per_unit", bufs=STAGE_2_LAG + 2))
+        per_step = ctx.enter_context(tc.tile_pool(name="per_step", bufs=STAGE_2_LAG + 2))
         results = ctx.enter_context(tc.tile_pool(name="results", bufs=6))
         psum = ctx.enter_context(tc.psum_pool(name="psum", bufs=PSUM_BANKS))
 
-        def copy_out(on_vector, dst, src):
+        def copy(on_vector, dst, src):
             if on_vector:
                 nc.vector.tensor_copy(out=dst, in_=src)
             else:
@@ -63,12 +67,12 @@ def tile_mpolinear2_pa_kernel(tc, t_first, mid_core0, mid_core1, out):
                     )
             x_tiles.append(x_tile)
 
-        w0_raw = keep.tile([P, PACK, COLS], BF16)
+        load_chunk(0, PAIR)
+        w0_raw = keep.tile([P, PAIR, PAIR * COLS], BF16)
         nc.sync.dma_start(
             out=w0_raw[:],
-            in_=mid_core0.rearrange("(t xl) r s p -> (xl r) t (s p)", t=PACK),
+            in_=mid_core0.rearrange("(u x) (r e) s p -> (x r) u (e s p)", u=PAIR, e=PAIR),
         )
-        load_chunk(0, 2)
         w1_raw = keep.tile([P, PACK, COLS], BF16)
         core1_rows = mid_core1.rearrange("(yh yl) s u q -> yh s yl (u q)", yl=PACK)
         for yh in range(Y_HALVES):
@@ -92,60 +96,52 @@ def tile_mpolinear2_pa_kernel(tc, t_first, mid_core0, mid_core1, out):
                 in_=ident[:, half].rearrange("i (y z b) -> i b z y", b=B_PAIR, z=SITE),
             )
 
-        w0_grouped = keep.tile([P, PHYS, BOND, PACK], BF16, align_bytes=64)
-        nc.vector.tensor_copy(
-            out=w0_grouped[:], in_=w0_raw[:].rearrange("c t (s p) -> c p s t", p=PHYS)
-        )
-        for p in range(PHYS):
-            cols = slice((2 * p + 1) * BOND, (2 * p + 2) * BOND)
-            nc.vector.quantize_mx(
-                out=w0_codes[:, cols].bitcast(FP8X4),
-                scales=w0_scales[:, cols],
-                in_=w0_grouped[:, p].rearrange("c s t -> c (s t)"),
-            )
-
-        w1_codes = keep.tile([P, COLS], U32, align_bytes=64)
-        w1_scales = keep.tile([P, COLS], U8, align_bytes=64)
-        w1_grouped = keep.tile([P, COLS, PACK], BF16, align_bytes=64)
-
-        def prepare_core1():
-            nc.vector.tensor_copy(out=w1_grouped[:], in_=w1_raw[:].rearrange("m l n -> m n l"))
-
-        def quantise_core1():
-            nc.vector.quantize_mx(
-                out=w1_codes[:].bitcast(FP8X4),
-                scales=w1_scales[:],
-                in_=w1_grouped[:].rearrange("m n l -> m (n l)"),
-            )
-
+        shuffled = {}
         a_grouped = {}
         a_codes = {}
         a_scales = {}
 
-        def transpose_run(chunk, run):
-            words = x_tiles[chunk][:].bitcast(F32).rearrange("g x (r w) -> g w (x r)", w=O_WORDS)
+        def shuffle(on_vector, chunk, oh, x_part, x_parts):
+            if chunk not in shuffled:
+                tile = per_chunk.tile([P, PHYS, COLS], BF16, align_bytes=64, name="shuffled")
+                shuffled[chunk] = tile
+            o_half = slice(O_RUN * oh, O_RUN * (oh + 1))
+            ks = slice(COLS // x_parts * x_part, COLS // x_parts * (x_part + 1))
+            copy(
+                on_vector,
+                shuffled[chunk][:, o_half, ks].rearrange("g o k -> g k o"),
+                x_tiles[chunk][:].rearrange("g x (r o) -> g (x r) o", o=PHYS)[:, ks, o_half],
+            )
+
+        def transpose_run(chunk, oh):
+            words = shuffled[chunk][:].bitcast(F32)
             banks = []
-            for i in range(RUN_BANKS):
-                bank = psum.tile([P, PACK, P], F32, tag="bank", name="bank")
+            for i in range(BANKS_PER_RUN):
+                bank = psum.tile([P, PAIR, PAIR, P], F32, tag="bank", name="bank")
                 banks.append(bank)
-            for t in range(PACK):
-                for i in range(RUN_BANKS):
-                    nc.tensor.transpose(
-                        banks[i][:, t, :], words[:, RUN_BANKS * run + i, t * P : (t + 1) * P], reorder[:]
-                    )
+            for u in range(PAIR):
+                for i in range(BANKS_PER_RUN):
+                    for oe in range(PAIR):
+                        nc.tensor.transpose(
+                            banks[i][:, oe, u, :],
+                            words[:, O_RUN * oh + PAIR * i + oe, u * P : (u + 1) * P],
+                            reorder[:],
+                        )
             return banks
 
-        def regroup_run(chunk, run, banks):
-            if run == 0:
+        def regroup_run(chunk, oh, banks, vector_banks):
+            if oh == 0:
                 grouped = per_chunk.tile(
-                    [P, Y_HALVES * BZ, O_WORDS, PACK * 2, PACK], BF16, align_bytes=64, name="a_grouped"
+                    [P, Y_HALVES * BZ, O_PAIRS, PACK * PAIR * PACK], BF16, align_bytes=64, name="a_grouped"
                 )
                 a_grouped[chunk] = grouped
-            for i in range(RUN_BANKS):
-                copy_out(
-                    i % 2 == 1,
-                    a_grouped[chunk][:, :, RUN_BANKS * run + i],
-                    banks[i][:].bitcast(BF16).rearrange("c t (h m) -> c h m t", m=PACK * 2),
+            for i in range(BANKS_PER_RUN):
+                copy(
+                    i >= BANKS_PER_RUN - vector_banks,
+                    a_grouped[chunk][:, :, BANKS_PER_RUN * oh + i]
+                    .bitcast(F32)
+                    .rearrange("c g (y v) -> c g y v", y=PACK),
+                    banks[i][:].rearrange("c o u (g y) -> c g y (o u)", y=PACK),
                 )
 
         def quantise_a(chunk, yh):
@@ -157,90 +153,134 @@ def tile_mpolinear2_pa_kernel(tc, t_first, mid_core0, mid_core1, out):
             nc.vector.quantize_mx(
                 out=a_codes[chunk][:, yh, :].bitcast(FP8X4),
                 scales=a_scales[chunk][:, yh, :],
-                in_=a_grouped[chunk][:, yh * BZ : (yh + 1) * BZ].rearrange("c b w m t -> c (b w m t)"),
+                in_=a_grouped[chunk][:, yh * BZ : (yh + 1) * BZ].rearrange("c b w k -> c (b w k)"),
+            )
+
+        w0_grouped = keep.tile([P, PHYS, BOND, PACK], BF16, align_bytes=64)
+        w1_codes = keep.tile([P, COLS], U32, align_bytes=64)
+        w1_scales = keep.tile([P, COLS], U8, align_bytes=64)
+        w1_grouped = keep.tile([P, COLS, PACK], BF16, align_bytes=64)
+
+        def regroup_core0():
+            nc.vector.tensor_copy(
+                out=w0_grouped[:],
+                in_=w0_raw[:].rearrange("c u (e s p) -> c p s (u e)", e=PAIR, p=PHYS),
+            )
+
+        def quantise_core0():
+            for p in range(PHYS):
+                cols = slice((2 * p + 1) * BOND, (2 * p + 2) * BOND)
+                nc.vector.quantize_mx(
+                    out=w0_codes[:, cols].bitcast(FP8X4),
+                    scales=w0_scales[:, cols],
+                    in_=w0_grouped[:, p].rearrange("c s t -> c (s t)"),
+                )
+
+        def regroup_core1():
+            nc.vector.tensor_copy(out=w1_grouped[:], in_=w1_raw[:].rearrange("m l n -> m n l"))
+
+        def quantise_core1():
+            nc.vector.quantize_mx(
+                out=w1_codes[:].bitcast(FP8X4),
+                scales=w1_scales[:],
+                in_=w1_grouped[:].rearrange("m n l -> m (n l)"),
             )
 
         t2_grouped = {}
         t2_codes = {}
         t2_scales = {}
-        result_tiles = {}
 
-        def stage_1(unit):
-            chunk, p = divmod(unit, PHYS)
-            bank = psum.tile([P, COLS], F32, tag="bank", name="bank")
-            for yh in range(Y_HALVES):
-                first = (2 * p + 1 - yh) * BOND
+        def stage_1(step):
+            chunk, pair = divmod(step, STEPS_PER_CHUNK)
+            grouped = per_step.tile([P, P_PAIR, COLS], BF16, align_bytes=64, name="t2_grouped")
+            for i in range(P_PAIR):
+                p = P_PAIR * pair + i
+                bank = psum.tile([P, COLS], F32, tag="bank", name="bank")
+                for yh in range(Y_HALVES):
+                    first = (2 * p + 1 - yh) * BOND
+                    nc.tensor.matmul_mx(
+                        out=bank[:],
+                        lhsT=w0_codes[:, first : first + P].bitcast(FP8X4),
+                        lhsT_scale=w0_scales[:, first : first + P],
+                        rhs=a_codes[chunk][:, yh, :].bitcast(FP8X4),
+                        rhs_scale=a_scales[chunk][:, yh, :],
+                        start=yh == 0,
+                        stop=yh == Y_HALVES - 1,
+                    )
+                nc.scalar.copy(
+                    out=grouped[:, i].rearrange("m (g e l) -> m g e l", e=PAIR, l=PACK),
+                    in_=bank[:].rearrange("m (g l e) -> m g e l", l=PACK, e=PAIR),
+                )
+            t2_grouped[step] = grouped
+
+        def quantise_t2(step):
+            codes = per_step.tile([P, P_PAIR, P], U32, align_bytes=64, name="t2_codes")
+            scales = per_step.tile([P, P_PAIR, P], U8, align_bytes=64, name="t2_scales")
+            nc.vector.quantize_mx(
+                out=codes[:].rearrange("m i n -> m (i n)").bitcast(FP8X4),
+                scales=scales[:].rearrange("m i n -> m (i n)"),
+                in_=t2_grouped[step][:].rearrange("m i n -> m (i n)"),
+            )
+            t2_codes[step] = codes
+            t2_scales[step] = scales
+
+        def stage_2(step):
+            chunk, pair = divmod(step, STEPS_PER_CHUNK)
+            result = results.tile([P, P_PAIR, COLS], F32, name="result")
+            for i in range(P_PAIR):
+                acc = psum.tile([P, COLS], F32, tag="bank", name="bank")
                 nc.tensor.matmul_mx(
-                    out=bank[:],
-                    lhsT=w0_codes[:, first : first + P].bitcast(FP8X4),
-                    lhsT_scale=w0_scales[:, first : first + P],
-                    rhs=a_codes[chunk][:, yh, :].bitcast(FP8X4),
-                    rhs_scale=a_scales[chunk][:, yh, :],
-                    start=yh == 0,
-                    stop=yh == Y_HALVES - 1,
+                    out=acc[:],
+                    lhsT=t2_codes[step][:, i].bitcast(FP8X4),
+                    lhsT_scale=t2_scales[step][:, i],
+                    rhs=w1_codes[:].bitcast(FP8X4),
+                    rhs_scale=w1_scales[:],
+                    start=True,
+                    stop=True,
                 )
-            grouped = per_unit.tile([P, COLS], BF16, align_bytes=64, name="t2_grouped")
-            nc.scalar.copy(
-                out=grouped[:].rearrange("m (g e l) -> m g e l", e=2, l=PACK),
-                in_=bank[:].rearrange("m (g l e) -> m g e l", l=PACK, e=2),
+                copy(i == 0, result[:, i, :], acc[:])
+            nc.sync.dma_start(
+                out=out[
+                    B_PAIR * chunk : B_PAIR * (chunk + 1), :, :, P_PAIR * pair : P_PAIR * (pair + 1)
+                ].rearrange("b z o p u q -> (b z o) (p u q)"),
+                in_=result[:].rearrange("m p n -> m (p n)"),
             )
-            t2_grouped[unit] = grouped
 
-        def quantise_t2(unit):
-            codes = per_unit.tile([P, P], U32, align_bytes=64, name="t2_codes")
-            scales = per_unit.tile([P, P], U8, align_bytes=64, name="t2_scales")
-            nc.vector.quantize_mx(out=codes[:].bitcast(FP8X4), scales=scales[:], in_=t2_grouped[unit][:])
-            t2_codes[unit] = codes
-            t2_scales[unit] = scales
+        for x_part in range(PAIR):
+            for oh in range(O_HALVES):
+                shuffle(oh == 0, 0, oh, x_part, PAIR)
+        first_banks = [transpose_run(0, oh) for oh in range(O_HALVES)]
+        regroup_core0()
+        for oh in range(O_HALVES):
+            regroup_run(0, oh, first_banks[oh], oh)
+        quantise_core0()
+        for yh in range(Y_HALVES):
+            quantise_a(0, yh)
+        shuffle(True, 1, 0, 0, 1)
 
-        def stage_2(unit):
-            chunk, p = divmod(unit, PHYS)
-            if p % 2 == 0:
-                result = results.tile([P, 2, COLS], F32, name="result")
-                result_tiles[unit // 2] = result
-            acc = psum.tile([P, COLS], F32, tag="bank", name="bank")
-            nc.tensor.matmul_mx(
-                out=acc[:],
-                lhsT=t2_codes[unit][:].bitcast(FP8X4),
-                lhsT_scale=t2_scales[unit][:],
-                rhs=w1_codes[:].bitcast(FP8X4),
-                rhs_scale=w1_scales[:],
-                start=True,
-                stop=True,
-            )
-            copy_out(p % 4 != 3, result_tiles[unit // 2][:, p % 2, :], acc[:])
-            if p % 2 == 1:
-                nc.sync.dma_start(
-                    out=out[B_PAIR * chunk : B_PAIR * (chunk + 1), :, :, p - 1 : p + 1].rearrange(
-                        "b z o p u q -> (b z o) (p u q)"
-                    ),
-                    in_=result_tiles[unit // 2][:].rearrange("m p n -> m (p n)"),
-                )
-
-        runs = O_WORDS // RUN_BANKS
-        first_banks = [transpose_run(0, run) for run in range(runs)]
-        for run in range(runs):
-            regroup_run(0, run, first_banks[run])
-        quantise_a(0, 0)
-        quantise_a(0, 1)
-        prepare_core1()
-        for unit in range(UNITS + STAGE_2_LAG):
-            chunk, p = divmod(unit, PHYS)
+        for step in range(STEPS + STAGE_2_LAG):
+            chunk, pair = divmod(step, STEPS_PER_CHUNK)
             has_next = chunk + 1 < CHUNKS
-            if p == 0 and chunk + LOADS_AHEAD < CHUNKS:
+            if pair == 0 and chunk + LOADS_AHEAD < CHUNKS:
                 load_chunk(chunk + LOADS_AHEAD, 1)
-            run, at = divmod(p, UNITS_PER_RUN)
-            if at == 0 and has_next:
-                banks = transpose_run(chunk + 1, run)
-            if 1 <= unit <= UNITS:
-                quantise_t2(unit - 1)
-            if unit == 1:
+            if step == 1:
                 quantise_core1()
-            if at == 0 and has_next:
-                regroup_run(chunk + 1, run, banks)
-            if unit < UNITS:
-                stage_1(unit)
-            if unit >= STAGE_2_LAG:
-                stage_2(unit - STAGE_2_LAG)
-            if UNITS_PER_RUN < p <= UNITS_PER_RUN + Y_HALVES and has_next:
-                quantise_a(chunk + 1, p - UNITS_PER_RUN - 1)
+            if step >= STAGE_2_LAG:
+                quantise_t2(step - STAGE_2_LAG)
+            if step < STEPS:
+                stage_1(step)
+            if pair == 0 and has_next:
+                shuffle(True, chunk + 1, 1, 0, 1)
+            if pair == 1 and chunk + 2 < CHUNKS:
+                shuffle(True, chunk + 2, 0, 0, 1)
+            if step == 0:
+                regroup_core1()
+            if pair == 0 and has_next:
+                regroup_run(chunk + 1, 0, transpose_run(chunk + 1, 0), 0)
+            if pair == 2 and has_next:
+                regroup_run(chunk + 1, 1, transpose_run(chunk + 1, 1), 1)
+            if pair == 3 and has_next:
+                for yh in range(Y_HALVES):
+                    quantise_a(chunk + 1, yh)
+            if step >= STAGE_2_LAG:
+                stage_2(step - STAGE_2_LAG)

@@ -30,7 +30,8 @@ BZ = B_PAIR * SITE
 P_PAIR = 2
 STEPS_PER_CHUNK = PHYS // P_PAIR
 STEPS = CHUNKS * STEPS_PER_CHUNK
-STAGE_2_LAG = 1
+GROUP_STEPS = 2
+STAGE_2_LAG = 3
 LOADS_AHEAD = 3
 
 FLOPS = 2 * 2 * (B * SITE * SITE * PHYS) * (SITE * BOND) * COLS
@@ -41,9 +42,10 @@ def tile_mpolinear2_pa_kernel(tc, t_first, mid_core0, mid_core1, out):
     with ExitStack() as ctx:
         ctx.enter_context(tc.manual_schedule())
         keep = ctx.enter_context(tc.tile_pool(name="keep", bufs=1))
+        loads = ctx.enter_context(tc.tile_pool(name="loads", bufs=LOADS_AHEAD + 1))
         per_chunk = ctx.enter_context(tc.tile_pool(name="per_chunk", bufs=2))
-        per_step = ctx.enter_context(tc.tile_pool(name="per_step", bufs=STAGE_2_LAG + 2))
-        results = ctx.enter_context(tc.tile_pool(name="results", bufs=6))
+        per_step = ctx.enter_context(tc.tile_pool(name="per_step", bufs=4))
+        results = ctx.enter_context(tc.tile_pool(name="results", bufs=24))
         psum = ctx.enter_context(tc.psum_pool(name="psum", bufs=PSUM_BANKS))
 
         def copy(on_vector, dst, src):
@@ -52,10 +54,10 @@ def tile_mpolinear2_pa_kernel(tc, t_first, mid_core0, mid_core1, out):
             else:
                 nc.scalar.copy(out=dst, in_=src)
 
-        x_tiles = []
+        x_tiles = {}
 
         def load_chunk(chunk, x_parts):
-            x_tile = keep.tile([P, SITE, COLS], BF16, name="x_tile%d" % chunk)
+            x_tile = loads.tile([P, SITE, COLS], BF16, name="x_tile")
             width = SITE // x_parts
             for first in range(0, SITE, width):
                 for bl in range(B_PAIR):
@@ -65,7 +67,7 @@ def tile_mpolinear2_pa_kernel(tc, t_first, mid_core0, mid_core1, out):
                             "x y z r o -> (y z) x (r o)"
                         ),
                     )
-            x_tiles.append(x_tile)
+            x_tiles[chunk] = x_tile
 
         load_chunk(0, PAIR)
         w0_raw = keep.tile([P, PAIR, PAIR * COLS], BF16)
@@ -79,6 +81,11 @@ def tile_mpolinear2_pa_kernel(tc, t_first, mid_core0, mid_core1, out):
             nc.sync.dma_start(out=w1_raw[yh * HALF : (yh + 1) * HALF], in_=core1_rows[yh])
         for chunk in range(1, LOADS_AHEAD):
             load_chunk(chunk, 1)
+
+        warm = keep.tile([P, PAIR], BF16)
+        nc.vector.memset(warm[:], 0.0)
+        warm_copy = keep.tile([P, PAIR], BF16)
+        nc.scalar.copy(out=warm_copy[:], in_=warm[:])
 
         w0_blocks = 2 * PHYS + 1
         w0_codes = keep.tile([P, w0_blocks * BOND], U32, align_bytes=64)
@@ -144,17 +151,19 @@ def tile_mpolinear2_pa_kernel(tc, t_first, mid_core0, mid_core1, out):
                     banks[i][:].rearrange("c o u (g y) -> c g y (o u)", y=PACK),
                 )
 
-        def quantise_a(chunk, yh):
-            if yh == 0:
-                codes = per_chunk.tile([P, Y_HALVES, COLS], U32, align_bytes=64, name="a_codes")
-                scales = per_chunk.tile([P, Y_HALVES, COLS], U8, align_bytes=64, name="a_scales")
-                a_codes[chunk] = codes
-                a_scales[chunk] = scales
-            nc.vector.quantize_mx(
-                out=a_codes[chunk][:, yh, :].bitcast(FP8X4),
-                scales=a_scales[chunk][:, yh, :],
-                in_=a_grouped[chunk][:, yh * BZ : (yh + 1) * BZ].rearrange("c b w k -> c (b w k)"),
-            )
+        def quantise_a(chunk, parts):
+            codes = per_chunk.tile([P, Y_HALVES, COLS], U32, align_bytes=64, name="a_codes")
+            scales = per_chunk.tile([P, Y_HALVES, COLS], U8, align_bytes=64, name="a_scales")
+            for part in range(parts):
+                h = slice(Y_HALVES // parts * part, Y_HALVES // parts * (part + 1))
+                g = slice(Y_HALVES * BZ // parts * part, Y_HALVES * BZ // parts * (part + 1))
+                nc.vector.quantize_mx(
+                    out=codes[:, h].rearrange("c h n -> c (h n)").bitcast(FP8X4),
+                    scales=scales[:, h].rearrange("c h n -> c (h n)"),
+                    in_=a_grouped[chunk][:, g].rearrange("c b w k -> c (b w k)"),
+                )
+            a_codes[chunk] = codes
+            a_scales[chunk] = scales
 
         w0_grouped = keep.tile([P, PHYS, BOND, PACK], BF16, align_bytes=64)
         w1_codes = keep.tile([P, COLS], U32, align_bytes=64)
@@ -192,7 +201,10 @@ def tile_mpolinear2_pa_kernel(tc, t_first, mid_core0, mid_core1, out):
 
         def stage_1(step):
             chunk, pair = divmod(step, STEPS_PER_CHUNK)
-            grouped = per_step.tile([P, P_PAIR, COLS], BF16, align_bytes=64, name="t2_grouped")
+            if step % GROUP_STEPS == 0:
+                grouped = per_step.tile([P, GROUP_STEPS, P_PAIR, COLS], BF16, align_bytes=64, name="t2_grouped")
+                t2_grouped[step // GROUP_STEPS] = grouped
+            grouped = t2_grouped[step // GROUP_STEPS][:, step % GROUP_STEPS]
             for i in range(P_PAIR):
                 p = P_PAIR * pair + i
                 bank = psum.tile([P, COLS], F32, tag="bank", name="bank")
@@ -211,18 +223,18 @@ def tile_mpolinear2_pa_kernel(tc, t_first, mid_core0, mid_core1, out):
                     out=grouped[:, i].rearrange("m (g e l) -> m g e l", e=PAIR, l=PACK),
                     in_=bank[:].rearrange("m (g l e) -> m g e l", l=PACK, e=PAIR),
                 )
-            t2_grouped[step] = grouped
 
-        def quantise_t2(step):
-            codes = per_step.tile([P, P_PAIR, P], U32, align_bytes=64, name="t2_codes")
-            scales = per_step.tile([P, P_PAIR, P], U8, align_bytes=64, name="t2_scales")
+        def quantise_t2(group):
+            codes = per_step.tile([P, GROUP_STEPS, P_PAIR, P], U32, align_bytes=64, name="t2_codes")
+            scales = per_step.tile([P, GROUP_STEPS, P_PAIR, P], U8, align_bytes=64, name="t2_scales")
             nc.vector.quantize_mx(
-                out=codes[:].rearrange("m i n -> m (i n)").bitcast(FP8X4),
-                scales=scales[:].rearrange("m i n -> m (i n)"),
-                in_=t2_grouped[step][:].rearrange("m i n -> m (i n)"),
+                out=codes[:].rearrange("m k i n -> m (k i n)").bitcast(FP8X4),
+                scales=scales[:].rearrange("m k i n -> m (k i n)"),
+                in_=t2_grouped[group][:].rearrange("m k i n -> m (k i n)"),
             )
-            t2_codes[step] = codes
-            t2_scales[step] = scales
+            for k in range(GROUP_STEPS):
+                t2_codes[GROUP_STEPS * group + k] = codes[:, k]
+                t2_scales[GROUP_STEPS * group + k] = scales[:, k]
 
         def stage_2(step):
             chunk, pair = divmod(step, STEPS_PER_CHUNK)
@@ -238,7 +250,7 @@ def tile_mpolinear2_pa_kernel(tc, t_first, mid_core0, mid_core1, out):
                     start=True,
                     stop=True,
                 )
-                copy(i == 0, result[:, i, :], acc[:])
+                copy(i == 0 or pair == 1, result[:, i, :], acc[:])
             nc.sync.dma_start(
                 out=out[
                     B_PAIR * chunk : B_PAIR * (chunk + 1), :, :, P_PAIR * pair : P_PAIR * (pair + 1)
@@ -254,8 +266,7 @@ def tile_mpolinear2_pa_kernel(tc, t_first, mid_core0, mid_core1, out):
         for oh in range(O_HALVES):
             regroup_run(0, oh, first_banks[oh], oh)
         quantise_core0()
-        for yh in range(Y_HALVES):
-            quantise_a(0, yh)
+        quantise_a(0, Y_HALVES)
         shuffle(True, 1, 0, 0, 1)
 
         for step in range(STEPS + STAGE_2_LAG):
@@ -265,22 +276,21 @@ def tile_mpolinear2_pa_kernel(tc, t_first, mid_core0, mid_core1, out):
                 load_chunk(chunk + LOADS_AHEAD, 1)
             if step == 1:
                 quantise_core1()
-            if step >= STAGE_2_LAG:
-                quantise_t2(step - STAGE_2_LAG)
+            if step % GROUP_STEPS == 0 and 0 < step <= STEPS:
+                quantise_t2(step // GROUP_STEPS - 1)
             if step < STEPS:
                 stage_1(step)
             if pair == 0 and has_next:
                 shuffle(True, chunk + 1, 1, 0, 1)
-            if pair == 1 and chunk + 2 < CHUNKS:
+            if pair == 3 and chunk + 2 < CHUNKS:
                 shuffle(True, chunk + 2, 0, 0, 1)
             if step == 0:
                 regroup_core1()
             if pair == 0 and has_next:
                 regroup_run(chunk + 1, 0, transpose_run(chunk + 1, 0), 0)
-            if pair == 2 and has_next:
+            if pair == 1 and has_next:
                 regroup_run(chunk + 1, 1, transpose_run(chunk + 1, 1), 1)
-            if pair == 3 and has_next:
-                for yh in range(Y_HALVES):
-                    quantise_a(chunk + 1, yh)
+            if pair == 2 and has_next:
+                quantise_a(chunk + 1, 1)
             if step >= STAGE_2_LAG:
                 stage_2(step - STAGE_2_LAG)

@@ -31,6 +31,7 @@ P_PAIR = 2
 STEPS_PER_CHUNK = PHYS // P_PAIR
 STEPS = CHUNKS * STEPS_PER_CHUNK
 GROUP_STEPS = 2
+ALONE_LAG = 2
 STAGE_2_LAG = 3
 LOADS_AHEAD = 3
 
@@ -176,8 +177,8 @@ def tile_mpolinear2_pa_kernel(tc, t_first, mid_core0, mid_core1, out):
                 in_=w0_raw[:].rearrange("c u (e s p) -> c p s (u e)", e=PAIR, p=PHYS),
             )
 
-        def quantise_core0():
-            for p in range(PHYS):
+        def quantise_core0(ps):
+            for p in ps:
                 cols = slice((2 * p + 1) * BOND, (2 * p + 2) * BOND)
                 nc.vector.quantize_mx(
                     out=w0_codes[:, cols].bitcast(FP8X4),
@@ -186,7 +187,7 @@ def tile_mpolinear2_pa_kernel(tc, t_first, mid_core0, mid_core1, out):
                 )
 
         def regroup_core1():
-            nc.vector.tensor_copy(out=w1_grouped[:], in_=w1_raw[:].rearrange("m l n -> m n l"))
+            nc.scalar.copy(out=w1_grouped[:], in_=w1_raw[:].rearrange("m l n -> m n l"))
 
         def quantise_core1():
             nc.vector.quantize_mx(
@@ -199,12 +200,21 @@ def tile_mpolinear2_pa_kernel(tc, t_first, mid_core0, mid_core1, out):
         t2_codes = {}
         t2_scales = {}
 
+        def alone(step):
+            return step < STEPS_PER_CHUNK or step >= STEPS - STEPS_PER_CHUNK
+
+        def group_of(step):
+            if alone(step):
+                return step, 1
+            return step // GROUP_STEPS * GROUP_STEPS, GROUP_STEPS
+
         def stage_1(step):
             chunk, pair = divmod(step, STEPS_PER_CHUNK)
-            if step % GROUP_STEPS == 0:
+            first, count = group_of(step)
+            if step == first:
                 grouped = per_step.tile([P, GROUP_STEPS, P_PAIR, COLS], BF16, align_bytes=64, name="t2_grouped")
-                t2_grouped[step // GROUP_STEPS] = grouped
-            grouped = t2_grouped[step // GROUP_STEPS][:, step % GROUP_STEPS]
+                t2_grouped[first] = grouped
+            grouped = t2_grouped[first][:, step - first]
             for i in range(P_PAIR):
                 p = P_PAIR * pair + i
                 bank = psum.tile([P, COLS], F32, tag="bank", name="bank")
@@ -224,17 +234,17 @@ def tile_mpolinear2_pa_kernel(tc, t_first, mid_core0, mid_core1, out):
                     in_=bank[:].rearrange("m (g l e) -> m g e l", l=PACK, e=PAIR),
                 )
 
-        def quantise_t2(group):
+        def quantise_t2(first, count):
             codes = per_step.tile([P, GROUP_STEPS, P_PAIR, P], U32, align_bytes=64, name="t2_codes")
             scales = per_step.tile([P, GROUP_STEPS, P_PAIR, P], U8, align_bytes=64, name="t2_scales")
             nc.vector.quantize_mx(
-                out=codes[:].rearrange("m k i n -> m (k i n)").bitcast(FP8X4),
-                scales=scales[:].rearrange("m k i n -> m (k i n)"),
-                in_=t2_grouped[group][:].rearrange("m k i n -> m (k i n)"),
+                out=codes[:, 0:count].rearrange("m k i n -> m (k i n)").bitcast(FP8X4),
+                scales=scales[:, 0:count].rearrange("m k i n -> m (k i n)"),
+                in_=t2_grouped[first][:, 0:count].rearrange("m k i n -> m (k i n)"),
             )
-            for k in range(GROUP_STEPS):
-                t2_codes[GROUP_STEPS * group + k] = codes[:, k]
-                t2_scales[GROUP_STEPS * group + k] = scales[:, k]
+            for k in range(count):
+                t2_codes[first + k] = codes[:, k]
+                t2_scales[first + k] = scales[:, k]
 
         def stage_2(step):
             chunk, pair = divmod(step, STEPS_PER_CHUNK)
@@ -250,13 +260,17 @@ def tile_mpolinear2_pa_kernel(tc, t_first, mid_core0, mid_core1, out):
                     start=True,
                     stop=True,
                 )
-                copy(i == 0 or pair == 1, result[:, i, :], acc[:])
-            nc.sync.dma_start(
-                out=out[
-                    B_PAIR * chunk : B_PAIR * (chunk + 1), :, :, P_PAIR * pair : P_PAIR * (pair + 1)
-                ].rearrange("b z o p u q -> (b z o) (p u q)"),
-                in_=result[:].rearrange("m p n -> m (p n)"),
-            )
+                copy((i == 0 or pair == 1) and (chunk > 0 or i == 0), result[:, i, :], acc[:])
+            parts = P_PAIR if step == STEPS - 1 else 1
+            width = P_PAIR // parts
+            for first in range(0, P_PAIR, width):
+                ps = slice(P_PAIR * pair + first, P_PAIR * pair + first + width)
+                nc.sync.dma_start(
+                    out=out[B_PAIR * chunk : B_PAIR * (chunk + 1), :, :, ps].rearrange(
+                        "b z o p u q -> (b z o) (p u q)"
+                    ),
+                    in_=result[:, first : first + width].rearrange("m p n -> m (p n)"),
+                )
 
         for x_part in range(PAIR):
             for oh in range(O_HALVES):
@@ -265,32 +279,36 @@ def tile_mpolinear2_pa_kernel(tc, t_first, mid_core0, mid_core1, out):
         regroup_core0()
         for oh in range(O_HALVES):
             regroup_run(0, oh, first_banks[oh], oh)
-        quantise_core0()
+        quantise_core0(range(P_PAIR))
         quantise_a(0, Y_HALVES)
+        quantise_core0(range(P_PAIR, PHYS))
+        regroup_core1()
         shuffle(True, 1, 0, 0, 1)
 
-        for step in range(STEPS + STAGE_2_LAG):
+        stage_2_at = {}
+        for step in range(STEPS):
+            stage_2_at.setdefault(step + (ALONE_LAG if alone(step) else STAGE_2_LAG), []).append(step)
+        for step in range(STEPS + ALONE_LAG):
             chunk, pair = divmod(step, STEPS_PER_CHUNK)
             has_next = chunk + 1 < CHUNKS
             if pair == 0 and chunk + LOADS_AHEAD < CHUNKS:
                 load_chunk(chunk + LOADS_AHEAD, 1)
             if step == 1:
                 quantise_core1()
-            if step % GROUP_STEPS == 0 and 0 < step <= STEPS:
-                quantise_t2(step // GROUP_STEPS - 1)
+            if 0 < step <= STEPS:
+                first, count = group_of(step - 1)
+                if first + count == step:
+                    quantise_t2(first, count)
             if step < STEPS:
                 stage_1(step)
             if pair == 0 and has_next:
                 shuffle(True, chunk + 1, 1, 0, 1)
             if pair == 3 and chunk + 2 < CHUNKS:
                 shuffle(True, chunk + 2, 0, 0, 1)
-            if step == 0:
-                regroup_core1()
-            if pair == 0 and has_next:
-                regroup_run(chunk + 1, 0, transpose_run(chunk + 1, 0), 0)
             if pair == 1 and has_next:
-                regroup_run(chunk + 1, 1, transpose_run(chunk + 1, 1), 1)
+                for oh in range(O_HALVES):
+                    regroup_run(chunk + 1, oh, transpose_run(chunk + 1, oh), oh)
             if pair == 2 and has_next:
                 quantise_a(chunk + 1, 1)
-            if step >= STAGE_2_LAG:
-                stage_2(step - STAGE_2_LAG)
+            for earlier in stage_2_at.get(step, ()):
+                stage_2(earlier)

@@ -8,6 +8,7 @@ F32 = mybir.dt.float32
 U32 = mybir.dt.uint32
 U8 = mybir.dt.uint8
 FP8X4 = mybir.dt.float8_e4m3fn_x4
+ALU = mybir.AluOpType
 
 P = 128
 HALF = P // 2
@@ -24,6 +25,8 @@ O_HALVES = 2
 O_RUN = PHYS // O_HALVES
 O_PAIRS = PHYS // PAIR
 BANKS_PER_RUN = O_PAIRS // O_HALVES
+GPSIMD_O = 2
+GPSIMD_PIECES = PAIR * GPSIMD_O
 B_PAIR = 2
 CHUNKS = B // B_PAIR
 BZ = B_PAIR * SITE
@@ -113,12 +116,25 @@ def tile_mpolinear2_pa_kernel(tc, t_first, mid_core0, mid_core1, out):
             if chunk not in shuffled:
                 tile = per_chunk.tile([P, PHYS, COLS], BF16, align_bytes=64, name="shuffled")
                 shuffled[chunk] = tile
-            o_half = slice(O_RUN * oh, O_RUN * (oh + 1))
+            o_half = slice(O_RUN * oh, min(O_RUN * (oh + 1), PHYS if chunk < 2 else PHYS - GPSIMD_O))
             ks = slice(COLS // x_parts * x_part, COLS // x_parts * (x_part + 1))
             copy(
                 on_vector,
                 shuffled[chunk][:, o_half, ks].rearrange("g o k -> g k o"),
                 x_tiles[chunk][:].rearrange("g x (r o) -> g (x r) o", o=PHYS)[:, ks, o_half],
+            )
+
+        def shuffle_on_gpsimd(chunk, piece):
+            o, part = divmod(piece, PAIR)
+            o += PHYS - GPSIMD_O
+            ks = slice(COLS // PAIR * part, COLS // PAIR * (part + 1))
+            nc.gpsimd.tensor_scalar(
+                out=shuffled[chunk][:, o, ks],
+                in0=x_tiles[chunk][:].rearrange("g x (r o) -> g o (x r)", o=PHYS)[:, o, ks],
+                scalar1=1.0,
+                scalar2=0.0,
+                op0=ALU.mult,
+                op1=ALU.add,
             )
 
         def transpose_run(chunk, oh):
@@ -305,6 +321,8 @@ def tile_mpolinear2_pa_kernel(tc, t_first, mid_core0, mid_core1, out):
                 shuffle(True, chunk + 1, 1, 0, 1)
             if pair == 3 and chunk + 2 < CHUNKS:
                 shuffle(True, chunk + 2, 0, 0, 1)
+                for piece in range(GPSIMD_PIECES):
+                    shuffle_on_gpsimd(chunk + 2, piece)
             if pair == 1 and has_next:
                 for oh in range(O_HALVES):
                     regroup_run(chunk + 1, oh, transpose_run(chunk + 1, oh), oh)

@@ -92,8 +92,8 @@ def tile_mpolinear2_pa_kernel(tc, t_first, mid_core0, mid_core1, out):
         nc.scalar.copy(out=warm_copy[:], in_=warm[:])
 
         w0_blocks = 2 * PHYS + 1
-        w0_codes = keep.tile([P, w0_blocks * BOND], U32, align_bytes=64)
-        w0_scales = keep.tile([P, w0_blocks * BOND], U8, align_bytes=64)
+        w0_codes = keep.tile([P, w0_blocks * BOND], U32, align_bytes=256)
+        w0_scales = keep.tile([P, w0_blocks * BOND], U8, align_bytes=256)
         nc.vector.memset(w0_codes[:], 0)
         nc.vector.memset(w0_scales[:].bitcast(U32), 0)
 
@@ -114,7 +114,7 @@ def tile_mpolinear2_pa_kernel(tc, t_first, mid_core0, mid_core1, out):
 
         def shuffle(on_vector, chunk, oh, x_part, x_parts):
             if chunk not in shuffled:
-                tile = per_chunk.tile([P, PHYS, COLS], BF16, align_bytes=64, name="shuffled")
+                tile = per_chunk.tile([P, PHYS, COLS], BF16, align_bytes=256, name="shuffled")
                 shuffled[chunk] = tile
             o_half = slice(O_RUN * oh, min(O_RUN * (oh + 1), PHYS if chunk < 2 else PHYS - GPSIMD_O))
             ks = slice(COLS // x_parts * x_part, COLS // x_parts * (x_part + 1))
@@ -143,20 +143,22 @@ def tile_mpolinear2_pa_kernel(tc, t_first, mid_core0, mid_core1, out):
             for i in range(BANKS_PER_RUN):
                 bank = psum.tile([P, PAIR, PAIR, P], F32, tag="bank", name="bank")
                 banks.append(bank)
-            for u in range(PAIR):
-                for i in range(BANKS_PER_RUN):
-                    for oe in range(PAIR):
-                        nc.tensor.transpose(
-                            banks[i][:, oe, u, :],
-                            words[:, O_RUN * oh + PAIR * i + oe, u * P : (u + 1) * P],
-                            reorder[:],
-                        )
+            if chunk == 0:
+                order = [(u, i, oe) for u in range(PAIR) for i in range(BANKS_PER_RUN) for oe in range(PAIR)]
+            else:
+                order = [(u, i, oe) for i in range(BANKS_PER_RUN) for oe in range(PAIR) for u in range(PAIR)]
+            for u, i, oe in order:
+                nc.tensor.transpose(
+                    banks[i][:, oe, u, :],
+                    words[:, O_RUN * oh + PAIR * i + oe, u * P : (u + 1) * P],
+                    reorder[:],
+                )
             return banks
 
         def regroup_run(chunk, oh, banks, vector_banks):
             if oh == 0:
                 grouped = per_chunk.tile(
-                    [P, Y_HALVES * BZ, O_PAIRS, PACK * PAIR * PACK], BF16, align_bytes=64, name="a_grouped"
+                    [P, Y_HALVES * BZ, O_PAIRS, PACK * PAIR * PACK], BF16, align_bytes=256, name="a_grouped"
                 )
                 a_grouped[chunk] = grouped
             for i in range(BANKS_PER_RUN):
@@ -169,8 +171,8 @@ def tile_mpolinear2_pa_kernel(tc, t_first, mid_core0, mid_core1, out):
                 )
 
         def quantise_a(chunk, parts):
-            codes = per_chunk.tile([P, Y_HALVES, COLS], U32, align_bytes=64, name="a_codes")
-            scales = per_chunk.tile([P, Y_HALVES, COLS], U8, align_bytes=64, name="a_scales")
+            codes = per_chunk.tile([P, Y_HALVES, COLS], U32, align_bytes=256, name="a_codes")
+            scales = per_chunk.tile([P, Y_HALVES, COLS], U8, align_bytes=256, name="a_scales")
             for part in range(parts):
                 h = slice(Y_HALVES // parts * part, Y_HALVES // parts * (part + 1))
                 g = slice(Y_HALVES * BZ // parts * part, Y_HALVES * BZ // parts * (part + 1))
@@ -182,10 +184,10 @@ def tile_mpolinear2_pa_kernel(tc, t_first, mid_core0, mid_core1, out):
             a_codes[chunk] = codes
             a_scales[chunk] = scales
 
-        w0_grouped = keep.tile([P, PHYS, BOND, PACK], BF16, align_bytes=64)
-        w1_codes = keep.tile([P, COLS], U32, align_bytes=64)
-        w1_scales = keep.tile([P, COLS], U8, align_bytes=64)
-        w1_grouped = keep.tile([P, COLS, PACK], BF16, align_bytes=64)
+        w0_grouped = keep.tile([P, PHYS, BOND, PACK], BF16, align_bytes=256)
+        w1_codes = keep.tile([P, COLS], U32, align_bytes=256)
+        w1_scales = keep.tile([P, COLS], U8, align_bytes=256)
+        w1_grouped = keep.tile([P, COLS, PACK], BF16, align_bytes=256)
 
         def regroup_core0():
             nc.vector.tensor_copy(
@@ -228,7 +230,7 @@ def tile_mpolinear2_pa_kernel(tc, t_first, mid_core0, mid_core1, out):
             chunk, pair = divmod(step, STEPS_PER_CHUNK)
             first, count = group_of(step)
             if step == first:
-                grouped = per_step.tile([P, GROUP_STEPS, P_PAIR, COLS], BF16, align_bytes=64, name="t2_grouped")
+                grouped = per_step.tile([P, GROUP_STEPS, P_PAIR, COLS], BF16, align_bytes=256, name="t2_grouped")
                 t2_grouped[first] = grouped
             grouped = t2_grouped[first][:, step - first]
             for i in range(P_PAIR):
@@ -251,8 +253,8 @@ def tile_mpolinear2_pa_kernel(tc, t_first, mid_core0, mid_core1, out):
                 )
 
         def quantise_t2(first, count):
-            codes = per_step.tile([P, GROUP_STEPS, P_PAIR, P], U32, align_bytes=64, name="t2_codes")
-            scales = per_step.tile([P, GROUP_STEPS, P_PAIR, P], U8, align_bytes=64, name="t2_scales")
+            codes = per_step.tile([P, GROUP_STEPS, P_PAIR, P], U32, align_bytes=256, name="t2_codes")
+            scales = per_step.tile([P, GROUP_STEPS, P_PAIR, P], U8, align_bytes=256, name="t2_scales")
             nc.vector.quantize_mx(
                 out=codes[:, 0:count].rearrange("m k i n -> m (k i n)").bitcast(FP8X4),
                 scales=scales[:, 0:count].rearrange("m k i n -> m (k i n)"),
@@ -325,7 +327,7 @@ def tile_mpolinear2_pa_kernel(tc, t_first, mid_core0, mid_core1, out):
                     shuffle_on_gpsimd(chunk + 2, piece)
             if pair == 1 and has_next:
                 for oh in range(O_HALVES):
-                    regroup_run(chunk + 1, oh, transpose_run(chunk + 1, oh), oh)
+                    regroup_run(chunk + 1, oh, transpose_run(chunk + 1, oh), oh if chunk % 2 else 1)
             if pair == 2 and has_next:
                 quantise_a(chunk + 1, 1)
             for earlier in stage_2_at.get(step, ()):

@@ -103,7 +103,7 @@ def tile_mpolinear2_pa_kernel(tc, t_first, mid_core0, mid_core1, out):
         for yh in range(Y_HALVES):
             half = slice(yh * HALF, (yh + 1) * HALF)
             nc.vector.tensor_copy(
-                out=reorder[:, half].rearrange("i (b z y) -> i b z y", b=B_PAIR, z=SITE),
+                out=reorder[:].rearrange("i (y h b z) -> i h b z y", y=PACK, h=Y_HALVES, b=B_PAIR)[:, yh],
                 in_=ident[:, half].rearrange("i (y z b) -> i b z y", b=B_PAIR, z=SITE),
             )
 
@@ -141,7 +141,7 @@ def tile_mpolinear2_pa_kernel(tc, t_first, mid_core0, mid_core1, out):
             words = shuffled[chunk][:].bitcast(F32)
             banks = []
             for i in range(BANKS_PER_RUN):
-                bank = psum.tile([P, PAIR, PAIR, P], F32, tag="bank", name="bank")
+                bank = psum.tile([P, PAIR, PACK, PAIR, Y_HALVES * BZ], F32, tag="bank", name="bank")
                 banks.append(bank)
             if chunk == 0:
                 order = [(u, i, oe) for u in range(PAIR) for i in range(BANKS_PER_RUN) for oe in range(PAIR)]
@@ -149,7 +149,7 @@ def tile_mpolinear2_pa_kernel(tc, t_first, mid_core0, mid_core1, out):
                 order = [(u, i, oe) for i in range(BANKS_PER_RUN) for oe in range(PAIR) for u in range(PAIR)]
             for u, i, oe in order:
                 nc.tensor.transpose(
-                    banks[i][:, oe, u, :],
+                    banks[i][:, oe, :, u, :],
                     words[:, O_RUN * oh + PAIR * i + oe, u * P : (u + 1) * P],
                     reorder[:],
                 )
@@ -164,10 +164,8 @@ def tile_mpolinear2_pa_kernel(tc, t_first, mid_core0, mid_core1, out):
             for i in range(BANKS_PER_RUN):
                 copy(
                     i >= BANKS_PER_RUN - vector_banks,
-                    a_grouped[chunk][:, :, BANKS_PER_RUN * oh + i]
-                    .bitcast(F32)
-                    .rearrange("c g (y v) -> c g y v", y=PACK),
-                    banks[i][:].rearrange("c o u (g y) -> c g y (o u)", y=PACK),
+                    a_grouped[chunk][:, :, BANKS_PER_RUN * oh + i].bitcast(F32),
+                    banks[i][:].rearrange("c o y u g -> c g (o y u)"),
                 )
 
         def quantise_a(chunk, parts):
@@ -247,10 +245,7 @@ def tile_mpolinear2_pa_kernel(tc, t_first, mid_core0, mid_core1, out):
                         start=yh == 0,
                         stop=yh == Y_HALVES - 1,
                     )
-                nc.scalar.copy(
-                    out=grouped[:, i].rearrange("m (g e l) -> m g e l", e=PAIR, l=PACK),
-                    in_=bank[:].rearrange("m (g l e) -> m g e l", l=PACK, e=PAIR),
-                )
+                nc.scalar.copy(out=grouped[:, i], in_=bank[:])
 
         def quantise_t2(first, count):
             codes = per_step.tile([P, GROUP_STEPS, P_PAIR, P], U32, align_bytes=256, name="t2_codes")

@@ -36,6 +36,7 @@ STEPS = CHUNKS * STEPS_PER_CHUNK
 GROUP_STEPS = 2
 ALONE_LAG = 2
 STAGE_2_LAG = 3
+WARM_PASSES = 6
 LOADS_AHEAD = 3
 
 FLOPS = 2 * 2 * (B * SITE * SITE * PHYS) * (SITE * BOND) * COLS
@@ -73,7 +74,7 @@ def tile_mpolinear2_pa_kernel(tc, t_first, mid_core0, mid_core1, out):
                     )
             x_tiles[chunk] = x_tile
 
-        load_chunk(0, PAIR)
+        load_chunk(0, 4)
         w0_raw = keep.tile([P, PAIR, PAIR * COLS], BF16)
         nc.sync.dma_start(
             out=w0_raw[:],
@@ -106,6 +107,12 @@ def tile_mpolinear2_pa_kernel(tc, t_first, mid_core0, mid_core1, out):
                 out=reorder[:].rearrange("i (y h b z) -> i h b z y", y=PACK, h=Y_HALVES, b=B_PAIR)[:, yh],
                 in_=ident[:, half].rearrange("i (y z b) -> i b z y", b=B_PAIR, z=SITE),
             )
+
+        zeros = keep.tile([P, COLS], BF16)
+        nc.vector.memset(zeros[:], 0.0)
+        warm_bank = psum.tile([P, COLS], F32, tag="bank", name="bank")
+        for i in range(WARM_PASSES):
+            nc.tensor.matmul(out=warm_bank[:], lhsT=zeros[:, 0:P], rhs=zeros[:], start=True, stop=True)
 
         shuffled = {}
         a_grouped = {}
@@ -285,9 +292,9 @@ def tile_mpolinear2_pa_kernel(tc, t_first, mid_core0, mid_core1, out):
                     in_=result[:, first : first + width].rearrange("m p n -> m (p n)"),
                 )
 
-        for x_part in range(PAIR):
+        for x_part in range(4):
             for oh in range(O_HALVES):
-                shuffle(oh == 0, 0, oh, x_part, PAIR)
+                shuffle(oh == 0 or x_part >= 4, 0, oh, x_part, 4)
         first_banks = [transpose_run(0, oh) for oh in range(O_HALVES)]
         regroup_core0()
         for oh in range(O_HALVES):

@@ -110,9 +110,13 @@ def tile_mpolinear2_pa_kernel(tc, t_first, mid_core0, mid_core1, out):
 
         zeros = keep.tile([P, COLS], BF16)
         nc.vector.memset(zeros[:], 0.0)
-        warm_bank = psum.tile([P, COLS], F32, tag="bank", name="bank")
-        for i in range(WARM_PASSES):
-            nc.tensor.matmul(out=warm_bank[:], lhsT=zeros[:, 0:P], rhs=zeros[:], start=True, stop=True)
+
+        def keep_warm(passes):
+            bank = psum.tile([P, COLS], F32, tag="bank", name="bank")
+            for i in range(passes):
+                nc.tensor.matmul(out=bank[:], lhsT=zeros[:, 0:P], rhs=zeros[:], start=True, stop=True)
+
+        keep_warm(WARM_PASSES)
 
         shuffled = {}
         a_grouped = {}
@@ -224,7 +228,7 @@ def tile_mpolinear2_pa_kernel(tc, t_first, mid_core0, mid_core1, out):
         t2_scales = {}
 
         def alone(step):
-            return step < STEPS_PER_CHUNK or step >= STEPS - STEPS_PER_CHUNK
+            return step < STEPS_PER_CHUNK or step >= STEPS - 2 * STEPS_PER_CHUNK
 
         def group_of(step):
             if alone(step):
@@ -266,7 +270,7 @@ def tile_mpolinear2_pa_kernel(tc, t_first, mid_core0, mid_core1, out):
                 t2_codes[first + k] = codes[:, k]
                 t2_scales[first + k] = scales[:, k]
 
-        def stage_2(step):
+        def stage_2(step, now):
             chunk, pair = divmod(step, STEPS_PER_CHUNK)
             result = results.tile([P, P_PAIR, COLS], F32, name="result")
             for i in range(P_PAIR):
@@ -280,8 +284,9 @@ def tile_mpolinear2_pa_kernel(tc, t_first, mid_core0, mid_core1, out):
                     start=True,
                     stop=True,
                 )
-                copy((i == 0 or pair == 1) and (chunk > 0 or i == 0), result[:, i, :], acc[:])
-            parts = P_PAIR if step == STEPS - 1 else 1
+                on_vector = STEPS - STEPS_PER_CHUNK <= now < STEPS or ((i == 0 or pair == 1) and (chunk > 0 or i == 0))
+                copy(on_vector, result[:, i, :], acc[:])
+            parts = P_PAIR if chunk == CHUNKS - 1 else 1
             width = P_PAIR // parts
             for first in range(0, P_PAIR, width):
                 ps = slice(P_PAIR * pair + first, P_PAIR * pair + first + width)
@@ -296,6 +301,7 @@ def tile_mpolinear2_pa_kernel(tc, t_first, mid_core0, mid_core1, out):
             for oh in range(O_HALVES):
                 shuffle(oh == 0 or x_part >= 4, 0, oh, x_part, 4)
         first_banks = [transpose_run(0, oh) for oh in range(O_HALVES)]
+        keep_warm(8)
         regroup_core0()
         for oh in range(O_HALVES):
             regroup_run(0, oh, first_banks[oh], oh)
@@ -333,4 +339,4 @@ def tile_mpolinear2_pa_kernel(tc, t_first, mid_core0, mid_core1, out):
             if pair == 2 and has_next:
                 quantise_a(chunk + 1, 1)
             for earlier in stage_2_at.get(step, ()):
-                stage_2(earlier)
+                stage_2(earlier, step)

@@ -8,7 +8,6 @@ F32 = mybir.dt.float32
 U32 = mybir.dt.uint32
 U8 = mybir.dt.uint8
 FP8X4 = mybir.dt.float8_e4m3fn_x4
-ALU = mybir.AluOpType
 
 P = 128
 HALF = P // 2
@@ -25,8 +24,6 @@ O_HALVES = 2
 O_RUN = PHYS // O_HALVES
 O_PAIRS = PHYS // PAIR
 BANKS_PER_RUN = O_PAIRS // O_HALVES
-GPSIMD_O = 2
-GPSIMD_PIECES = PAIR * GPSIMD_O
 B_PAIR = 2
 CHUNKS = B // B_PAIR
 BZ = B_PAIR * SITE
@@ -127,25 +124,12 @@ def tile_mpolinear2_pa_kernel(tc, t_first, mid_core0, mid_core1, out):
             if chunk not in shuffled:
                 tile = per_chunk.tile([P, PHYS, COLS], BF16, align_bytes=256, name="shuffled")
                 shuffled[chunk] = tile
-            o_half = slice(O_RUN * oh, min(O_RUN * (oh + 1), PHYS if chunk < 2 else PHYS - GPSIMD_O))
+            o_half = slice(O_RUN * oh, O_RUN * (oh + 1))
             ks = slice(COLS // x_parts * x_part, COLS // x_parts * (x_part + 1))
             copy(
                 on_vector,
                 shuffled[chunk][:, o_half, ks].rearrange("g o k -> g k o"),
                 x_tiles[chunk][:].rearrange("g x (r o) -> g (x r) o", o=PHYS)[:, ks, o_half],
-            )
-
-        def shuffle_on_gpsimd(chunk, piece):
-            o, part = divmod(piece, PAIR)
-            o += PHYS - GPSIMD_O
-            ks = slice(COLS // PAIR * part, COLS // PAIR * (part + 1))
-            nc.gpsimd.tensor_scalar(
-                out=shuffled[chunk][:, o, ks],
-                in0=x_tiles[chunk][:].rearrange("g x (r o) -> g o (x r)", o=PHYS)[:, o, ks],
-                scalar1=1.0,
-                scalar2=0.0,
-                op0=ALU.mult,
-                op1=ALU.add,
             )
 
         def transpose_run(chunk, oh):
@@ -328,11 +312,13 @@ def tile_mpolinear2_pa_kernel(tc, t_first, mid_core0, mid_core1, out):
             if step < STEPS:
                 stage_1(step)
             if pair == 0 and has_next:
-                shuffle(True, chunk + 1, 1, 0, 1)
+                for part in range(PAIR) if chunk == 0 else (1,):
+                    shuffle(True, chunk + 1, 1, part, PAIR)
+            if pair == 1 and chunk + 2 < CHUNKS:
+                shuffle(True, chunk + 2, 0, 0, PAIR)
             if pair == 3 and chunk + 2 < CHUNKS:
-                shuffle(True, chunk + 2, 0, 0, 1)
-                for piece in range(GPSIMD_PIECES):
-                    shuffle_on_gpsimd(chunk + 2, piece)
+                shuffle(True, chunk + 2, 0, 1, PAIR)
+                shuffle(True, chunk + 2, 1, 0, PAIR)
             if pair == 1 and has_next:
                 for oh in range(O_HALVES):
                     regroup_run(chunk + 1, oh, transpose_run(chunk + 1, oh), oh if chunk % 2 else 1)

from contextlib import ExitStack

import concourse.mybir as mybir
from concourse.masks import make_identity

BF16 = mybir.dt.bfloat16
F32 = mybir.dt.float32
U32 = mybir.dt.uint32
U8 = mybir.dt.uint8
FP8X4 = mybir.dt.float8_e4m3fn_x4

P = 128
HALF = P // 2
PACK = 4
PAIR = 2
B = 16
SITE = 8
BOND = 64
PHYS = 8
COLS = BOND * PHYS
PSUM_BANKS = 8
Y_HALVES = SITE // PACK
O_HALVES = 2
O_RUN = PHYS // O_HALVES
O_PAIRS = PHYS // PAIR
BANKS_PER_RUN = O_PAIRS // O_HALVES
B_PAIR = 2
CHUNKS = B // B_PAIR
BZ = B_PAIR * SITE
P_PAIR = 2
STEPS_PER_CHUNK = PHYS // P_PAIR
STEPS = CHUNKS * STEPS_PER_CHUNK
GROUP_STEPS = 2
ALONE_LAG = 2
STAGE_2_LAG = 3
WARM_PASSES = 6
LOADS_AHEAD = 3

FLOPS = 2 * 2 * (B * SITE * SITE * PHYS) * (SITE * BOND) * COLS


def tile_mpolinear2_pa_kernel(tc, t_first, mid_core0, mid_core1, out):
    nc = tc.nc
    with ExitStack() as ctx:
        ctx.enter_context(tc.manual_schedule())
        keep = ctx.enter_context(tc.tile_pool(name="keep", bufs=1))
        loads = ctx.enter_context(tc.tile_pool(name="loads", bufs=LOADS_AHEAD + 1))
        per_chunk = ctx.enter_context(tc.tile_pool(name="per_chunk", bufs=2))
        per_step = ctx.enter_context(tc.tile_pool(name="per_step", bufs=4))
        results = ctx.enter_context(tc.tile_pool(name="results", bufs=24))
        psum = ctx.enter_context(tc.psum_pool(name="psum", bufs=PSUM_BANKS))

        def copy(on_vector, dst, src):
            if on_vector:
                nc.vector.tensor_copy(out=dst, in_=src)
            else:
                nc.scalar.copy(out=dst, in_=src)

        x_tiles = {}

        def load_chunk(chunk, x_parts):
            x_tile = loads.tile([P, SITE, COLS], BF16, name="x_tile")
            width = SITE // x_parts
            for first in range(0, SITE, width):
                for bl in range(B_PAIR):
                    nc.sync.dma_start(
                        out=x_tile[bl:P:B_PAIR, first : first + width],
                        in_=t_first[B_PAIR * chunk + bl, first : first + width].rearrange(
                            "x y z r o -> (y z) x (r o)"
                        ),
                    )
            x_tiles[chunk] = x_tile

        load_chunk(0, 4)
        w0_raw = keep.tile([P, PAIR, PAIR * COLS], BF16)
        nc.sync.dma_start(
            out=w0_raw[:],
            in_=mid_core0.rearrange("(u x) (r e) s p -> (x r) u (e s p)", u=PAIR, e=PAIR),
        )
        w1_raw = keep.tile([P, PACK, COLS], BF16)
        core1_rows = mid_core1.rearrange("(yh yl) s u q -> yh s yl (u q)", yl=PACK)
        for yh in range(Y_HALVES):
            nc.sync.dma_start(out=w1_raw[yh * HALF : (yh + 1) * HALF], in_=core1_rows[yh])
        for chunk in range(1, LOADS_AHEAD):
            load_chunk(chunk, 1)

        warm = keep.tile([P, PAIR], BF16)
        nc.vector.memset(warm[:], 0.0)
        warm_copy = keep.tile([P, PAIR], BF16)
        nc.scalar.copy(out=warm_copy[:], in_=warm[:])

        w0_blocks = 2 * PHYS + 1
        w0_codes = keep.tile([P, w0_blocks * BOND], U32, align_bytes=256)
        w0_scales = keep.tile([P, w0_blocks * BOND], U8, align_bytes=256)
        nc.vector.memset(w0_codes[:], 0)
        nc.vector.memset(w0_scales[:].bitcast(U32), 0)

        ident = keep.tile([P, P], F32)
        make_identity(nc, ident[:])
        reorder = keep.tile([P, P], F32)
        for yh in range(Y_HALVES):
            half = slice(yh * HALF, (yh + 1) * HALF)
            nc.vector.tensor_copy(
                out=reorder[:].rearrange("i (y h b z) -> i h b z y", y=PACK, h=Y_HALVES, b=B_PAIR)[:, yh],
                in_=ident[:, half].rearrange("i (y z b) -> i b z y", b=B_PAIR, z=SITE),
            )

        zeros = keep.tile([P, COLS], BF16)
        nc.vector.memset(zeros[:], 0.0)

        def keep_warm(passes):
            bank = psum.tile([P, COLS], F32, tag="bank", name="bank")
            for i in range(passes):
                nc.tensor.matmul(out=bank[:], lhsT=zeros[:, 0:P], rhs=zeros[:], start=True, stop=True)

        keep_warm(WARM_PASSES)

        shuffled = {}
        a_grouped = {}
        a_codes = {}
        a_scales = {}

        def shuffle(on_vector, chunk, oh, x_part, x_parts):
            if chunk not in shuffled:
                tile = per_chunk.tile([P, PHYS, COLS], BF16, align_bytes=256, name="shuffled")
                shuffled[chunk] = tile
            o_half = slice(O_RUN * oh, O_RUN * (oh + 1))
            ks = slice(COLS // x_parts * x_part, COLS // x_parts * (x_part + 1))
            copy(
                on_vector,
                shuffled[chunk][:, o_half, ks].rearrange("g o k -> g k o"),
                x_tiles[chunk][:].rearrange("g x (r o) -> g (x r) o", o=PHYS)[:, ks, o_half],
            )

        def transpose_run(chunk, oh):
            words = shuffled[chunk][:].bitcast(F32)
            banks = []
            for i in range(BANKS_PER_RUN):
                bank = psum.tile([P, PAIR, PACK, PAIR, Y_HALVES * BZ], F32, tag="bank", name="bank")
                banks.append(bank)
            if chunk == 0:
                order = [(u, i, oe) for u in range(PAIR) for i in range(BANKS_PER_RUN) for oe in range(PAIR)]
            else:
                order = [(u, i, oe) for i in range(BANKS_PER_RUN) for oe in range(PAIR) for u in range(PAIR)]
            for u, i, oe in order:
                nc.tensor.transpose(
                    banks[i][:, oe, :, u, :],
                    words[:, O_RUN * oh + PAIR * i + oe, u * P : (u + 1) * P],
                    reorder[:],
                )
            return banks

        def regroup_run(chunk, oh, banks, vector_banks):
            if oh == 0:
                grouped = per_chunk.tile(
                    [P, Y_HALVES * BZ, O_PAIRS, PACK * PAIR * PACK], BF16, align_bytes=256, name="a_grouped"
                )
                a_grouped[chunk] = grouped
            for i in range(BANKS_PER_RUN):
                copy(
                    i >= BANKS_PER_RUN - vector_banks,
                    a_grouped[chunk][:, :, BANKS_PER_RUN * oh + i].bitcast(F32),
                    banks[i][:].rearrange("c o y u g -> c g (o y u)"),
                )

        def quantise_a(chunk, parts):
            codes = per_chunk.tile([P, Y_HALVES, COLS], U32, align_bytes=256, name="a_codes")
            scales = per_chunk.tile([P, Y_HALVES, COLS], U8, align_bytes=256, name="a_scales")
            for part in range(parts):
                h = slice(Y_HALVES // parts * part, Y_HALVES // parts * (part + 1))
                g = slice(Y_HALVES * BZ // parts * part, Y_HALVES * BZ // parts * (part + 1))
                nc.vector.quantize_mx(
                    out=codes[:, h].rearrange("c h n -> c (h n)").bitcast(FP8X4),
                    scales=scales[:, h].rearrange("c h n -> c (h n)"),
                    in_=a_grouped[chunk][:, g].rearrange("c b w k -> c (b w k)"),
                )
            a_codes[chunk] = codes
            a_scales[chunk] = scales

        w0_grouped = keep.tile([P, PHYS, BOND, PACK], BF16, align_bytes=256)
        w1_codes = keep.tile([P, COLS], U32, align_bytes=256)
        w1_scales = keep.tile([P, COLS], U8, align_bytes=256)
        w1_grouped = keep.tile([P, COLS, PACK], BF16, align_bytes=256)

        def regroup_core0():
            nc.vector.tensor_copy(
                out=w0_grouped[:],
                in_=w0_raw[:].rearrange("c u (e s p) -> c p s (u e)", e=PAIR, p=PHYS),
            )

        def quantise_core0(ps):
            for p in ps:
                cols = slice((2 * p + 1) * BOND, (2 * p + 2) * BOND)
                nc.vector.quantize_mx(
                    out=w0_codes[:, cols].bitcast(FP8X4),
                    scales=w0_scales[:, cols],
                    in_=w0_grouped[:, p].rearrange("c s t -> c (s t)"),
                )

        def regroup_core1():
            nc.scalar.copy(out=w1_grouped[:], in_=w1_raw[:].rearrange("m l n -> m n l"))

        def quantise_core1():
            nc.vector.quantize_mx(
                out=w1_codes[:].bitcast(FP8X4),
                scales=w1_scales[:],
                in_=w1_grouped[:].rearrange("m n l -> m (n l)"),
            )

        t2_grouped = {}
        t2_codes = {}
        t2_scales = {}

        def alone(step):
            return step < STEPS_PER_CHUNK or step >= STEPS - 2 * STEPS_PER_CHUNK

        def group_of(step):
            if alone(step):
                return step, 1
            return step // GROUP_STEPS * GROUP_STEPS, GROUP_STEPS

        def stage_1(step):
            chunk, pair = divmod(step, STEPS_PER_CHUNK)
            first, count = group_of(step)
            if step == first:
                grouped = per_step.tile([P, GROUP_STEPS, P_PAIR, COLS], BF16, align_bytes=256, name="t2_grouped")
                t2_grouped[first] = grouped
            grouped = t2_grouped[first][:, step - first]
            for i in range(P_PAIR):
                p = P_PAIR * pair + i
                bank = psum.tile([P, COLS], F32, tag="bank", name="bank")
                for yh in range(Y_HALVES):
                    first = (2 * p + 1 - yh) * BOND
                    nc.tensor.matmul_mx(
                        out=bank[:],
                        lhsT=w0_codes[:, first : first + P].bitcast(FP8X4),
                        lhsT_scale=w0_scales[:, first : first + P],
                        rhs=a_codes[chunk][:, yh, :].bitcast(FP8X4),
                        rhs_scale=a_scales[chunk][:, yh, :],
                        start=yh == 0,
                        stop=yh == Y_HALVES - 1,
                    )
                nc.scalar.copy(out=grouped[:, i], in_=bank[:])

        def quantise_t2(first, count):
            codes = per_step.tile([P, GROUP_STEPS, P_PAIR, P], U32, align_bytes=256, name="t2_codes")
            scales = per_step.tile([P, GROUP_STEPS, P_PAIR, P], U8, align_bytes=256, name="t2_scales")
            nc.vector.quantize_mx(
                out=codes[:, 0:count].rearrange("m k i n -> m (k i n)").bitcast(FP8X4),
                scales=scales[:, 0:count].rearrange("m k i n -> m (k i n)"),
                in_=t2_grouped[first][:, 0:count].rearrange("m k i n -> m (k i n)"),
            )
            for k in range(count):
                t2_codes[first + k] = codes[:, k]
                t2_scales[first + k] = scales[:, k]

        def stage_2(step, now):
            chunk, pair = divmod(step, STEPS_PER_CHUNK)
            result = results.tile([P, P_PAIR, COLS], F32, name="result")
            for i in range(P_PAIR):
                acc = psum.tile([P, COLS], F32, tag="bank", name="bank")
                nc.tensor.matmul_mx(
                    out=acc[:],
                    lhsT=t2_codes[step][:, i].bitcast(FP8X4),
                    lhsT_scale=t2_scales[step][:, i],
                    rhs=w1_codes[:].bitcast(FP8X4),
                    rhs_scale=w1_scales[:],
                    start=True,
                    stop=True,
                )
                on_vector = STEPS - STEPS_PER_CHUNK <= now < STEPS or ((i == 0 or pair == 1) and (chunk > 0 or i == 0))
                copy(on_vector, result[:, i, :], acc[:])
            parts = P_PAIR if chunk == CHUNKS - 1 else 1
            width = P_PAIR // parts
            for first in range(0, P_PAIR, width):
                ps = slice(P_PAIR * pair + first, P_PAIR * pair + first + width)
                nc.sync.dma_start(
                    out=out[B_PAIR * chunk : B_PAIR * (chunk + 1), :, :, ps].rearrange(
                        "b z o p u q -> (b z o) (p u q)"
                    ),
                    in_=result[:, first : first + width].rearrange("m p n -> m (p n)"),
                )

        for x_part in range(4):
            for oh in range(O_HALVES):
                shuffle(oh == 0 or x_part >= 4, 0, oh, x_part, 4)
        first_banks = [transpose_run(0, oh) for oh in range(O_HALVES)]
        keep_warm(8)
        regroup_core0()
        for oh in range(O_HALVES):
            regroup_run(0, oh, first_banks[oh], oh)
        quantise_core0(range(P_PAIR))
        quantise_a(0, Y_HALVES)
        quantise_core0(range(P_PAIR, PHYS))
        regroup_core1()
        shuffle(True, 1, 0, 0, 1)

        stage_2_at = {}
        for step in range(STEPS):
            stage_2_at.setdefault(step + (ALONE_LAG if alone(step) else STAGE_2_LAG), []).append(step)
        for step in range(STEPS + ALONE_LAG):
            chunk, pair = divmod(step, STEPS_PER_CHUNK)
            has_next = chunk + 1 < CHUNKS
            if pair == 0 and chunk + LOADS_AHEAD < CHUNKS:
                load_chunk(chunk + LOADS_AHEAD, 1)
            if step == 1:
                quantise_core1()
            if 0 < step <= STEPS:
                first, count = group_of(step - 1)
                if first + count == step:
                    quantise_t2(first, count)
            if step < STEPS:
                stage_1(step)
            if pair == 0 and has_next:
                for part in range(PAIR) if chunk == 0 else (1,):
                    shuffle(True, chunk + 1, 1, part, PAIR)
            if pair == 1 and chunk + 2 < CHUNKS:
                shuffle(True, chunk + 2, 0, 0, PAIR)
            if pair == 3 and chunk + 2 < CHUNKS:
                shuffle(True, chunk + 2, 0, 1, PAIR)
                shuffle(True, chunk + 2, 1, 0, PAIR)
            if pair == 1 and has_next:
                for oh in range(O_HALVES):
                    regroup_run(chunk + 1, oh, transpose_run(chunk + 1, oh), oh if chunk % 2 else 1)
            if pair == 2 and has_next:
                quantise_a(chunk + 1, 1)
            for earlier in stage_2_at.get(step, ()):
                stage_2(earlier, step)
